import numpy as np
import ml_dtypes


def mxq(x, axis, fmt="e4m3"):
    dtype, down = {"e4m3": (ml_dtypes.float8_e4m3fn, 7), "e5m2": (ml_dtypes.float8_e5m2, 14)}[fmt]
    v = np.moveaxis(np.asarray(x, np.float32).astype(ml_dtypes.bfloat16).astype(np.float64), axis, -1)
    blocks = v.reshape(v.shape[:-1] + (-1, 32))
    amax = np.abs(blocks).max(-1, keepdims=True)
    byte = np.maximum(np.where(amax > 0, np.frexp(amax)[1] - 1 + 127, 0) - down, 1)
    scale = np.exp2(byte - 127.0)
    codes = (blocks / scale).astype(np.float32).astype(dtype).astype(np.float64)
    return np.moveaxis((codes * scale).reshape(v.shape), -1, axis)


WIDE = False


def mx_kscale(k):
    if not WIDE:
        return np.ones(k)
    levels = np.array([10, -10, 5, -5, 0])
    a = np.random.permutation(np.resize(levels, k // 512 * 4)).reshape(k // 512, 4)
    idx = np.arange(k)
    return np.exp2(a[idx // 512, idx % 128 // 32])


BF16 = ml_dtypes.bfloat16


def bf(x):
    return np.asarray(x, np.float32).astype(BF16)


def f64(x):
    return np.asarray(x).astype(np.float64)


B, S, H, D = 1, 512, 16, 128
HD = H * D
LAYER_NUMBER = 2.0
NORM_FACTOR = LAYER_NUMBER * np.sqrt(D)


def setup_inputs():
    s = mx_kscale(HD)
    return {
        "hidden_states": bf(np.random.standard_normal((B, S, HD)) * s),
        "W_value": bf(np.random.standard_normal((HD, HD)) / np.sqrt(HD) / s[:, None]),
        "b_value": bf(np.random.standard_normal(HD) * 0.1),
        "query": bf(np.random.standard_normal((B, H, S, D))),
        "key": bf(np.random.standard_normal((B, H, S, D))),
        "alibi": bf(np.random.standard_normal((B, H, S))[:, :, None, :]),
        "attention_mask": bf(np.random.standard_normal((B, S, S))[:, None, :, :]),
    }


def reference(hidden_states, W_value, b_value, query, key, alibi, attention_mask):
    v = (mxq(f64(hidden_states), 2, "e4m3") @ mxq(f64(W_value), 0, "e4m3")) + f64(b_value)
    value = v.reshape(B, S, H, D).transpose(0, 2, 1, 3)
    scores = f64(query) @ f64(key).transpose(0, 1, 3, 2) / NORM_FACTOR
    scores = scores + f64(alibi) / LAYER_NUMBER
    scores = scores * LAYER_NUMBER + f64(attention_mask)
    e = np.exp(scores - scores.max(-1, keepdims=True))
    context = (mxq(e, 3, "e4m3") @ mxq(value, 2, "e4m3")) / e.sum(-1, keepdims=True)
    return context.transpose(0, 2, 1, 3).reshape(B, S, HD)

@@ -1,0 +1,387 @@
+import math
+from contextlib import ExitStack
+
+import concourse.mybir as mybir
+from concourse.masks import make_identity
+
+F32 = mybir.dt.float32
+BF16 = mybir.dt.bfloat16
+U8 = mybir.dt.uint8
+U32 = mybir.dt.uint32
+FP8X4 = mybir.dt.float8_e4m3fn_x4
+ALU = mybir.AluOpType
+ACT = mybir.ActivationFunctionType
+AXIS_X = mybir.AxisListType.X
+
+P = 128
+PACK = 4
+K_PASS = P * PACK
+
+SEQ = 512
+HEADS = 16
+HEAD_DIM = 128
+HIDDEN = HEADS * HEAD_DIM
+BLOCKS = SEQ // P
+PASSES = HIDDEN // K_PASS
+GROUP = 4
+GROUPS = HEADS // GROUP
+GROUP_COLS = GROUP * HEAD_DIM
+
+SCALE = 1.0 / math.sqrt(HEAD_DIM)
+INV_SCALE = math.sqrt(HEAD_DIM)
+
+LAG_TRANSPOSE = 1
+LAG_VALUE = 2
+LAG_CONTEXT = 3
+HIDDEN_STATES_STEP = 1
+
+FLOPS = 2 * SEQ * HIDDEN * HIDDEN + 2 * (2 * HEADS * SEQ * SEQ * HEAD_DIM)
+
+
+def tile_fastbloomattention_pa_kernel(
+    tc, hidden_states, W_value, b_value, query, key, alibi, attention_mask, out
+):
+    nc = tc.nc
+
+    mask_rows = attention_mask.rearrange("a b i j -> (a b i) j").rearrange("(p ib) j -> p ib j", ib=BLOCKS)
+    q_rows = query.rearrange("b h i d -> (b h) i d").rearrange("h (p ib) d -> p h (ib d)", ib=BLOCKS)
+    k_rows = key.rearrange("b h j d -> (b h j) d").rearrange("(x p) d -> p x d", p=P)
+    alibi_rows = alibi.rearrange("b h o j -> (b h o j)").rearrange("(x p) -> x p", p=P)
+    hs_rows = hidden_states.rearrange("b i k -> (b i) k").rearrange("(t p) k -> p t k", p=P)
+    w_rows = W_value.rearrange("(gu p e) n -> p gu e n", p=P, e=2)
+    out_rows = out.rearrange("b i n -> (b i) n").rearrange("(p ib) n -> p ib n", ib=BLOCKS)
+
+    with ExitStack() as stack:
+        const = stack.enter_context(tc.tile_pool(name="const", bufs=1))
+        weights = stack.enter_context(tc.tile_pool(name="weights", bufs=3))
+        work = stack.enter_context(tc.tile_pool(name="work", bufs=2))
+        stats = stack.enter_context(tc.tile_pool(name="stats", bufs=LAG_CONTEXT + 1))
+        psum = stack.enter_context(tc.psum_pool(name="psum", bufs=1))
+
+        def score_bank(shape):
+            return psum.tile(shape, F32, name="score_bank", tag="score_bank", bufs=3)
+
+        def transpose_bank(shape):
+            return psum.tile(shape, BF16, name="transpose_bank", tag="transpose_bank", bufs=3)
+
+        def head_cols(h):
+            return slice((h % GROUP) * HEAD_DIM, (h % GROUP + 1) * HEAD_DIM)
+
+        mask_sb = const.tile([P, BLOCKS, SEQ], BF16)
+        nc.sync.dma_start(out=mask_sb[:], in_=mask_rows)
+        alibi_sb = const.tile([P, P], BF16)
+        nc.vector.memset(alibi_sb[:], 0.0)
+        nc.sync.dma_start(out=alibi_sb[0 : HEADS * BLOCKS, :], in_=alibi_rows)
+
+        q_sb = const.tile([P, HEADS, BLOCKS * HEAD_DIM], BF16)
+        k_sb = const.tile([P, HEADS * BLOCKS, HEAD_DIM], BF16)
+
+        def load_query_and_key(group):
+            heads = slice(group * GROUP, (group + 1) * GROUP)
+            blocks = slice(group * GROUP * BLOCKS, (group + 1) * GROUP * BLOCKS)
+            nc.sync.dma_start(out=q_sb[:, heads, :], in_=q_rows[:, heads, :])
+            nc.sync.dma_start(out=k_sb[:, blocks, :], in_=k_rows[:, blocks, :])
+
+        w_raw_of = {}
+
+        def load_w(group):
+            w_raw = weights.tile([P, PASSES, PACK, GROUP_COLS], BF16, name="w_raw", tag="w_raw")
+            cols = slice(group * GROUP_COLS, (group + 1) * GROUP_COLS)
+            for g in range(PASSES):
+                for u in range(2):
+                    nc.sync.dma_start(
+                        out=w_raw[:, g, 2 * u : 2 * u + 2, :], in_=w_rows[:, 2 * g + u, :, cols]
+                    )
+            w_raw_of[group] = w_raw
+
+        load_query_and_key(0)
+        load_w(0)
+        hs_sb = const.tile([P, BLOCKS, HIDDEN], BF16)
+        nc.sync.dma_start(out=hs_sb[:], in_=hs_rows)
+        bias_sb = const.tile([P, HIDDEN], BF16)
+        nc.sync.dma_start(out=bias_sb[:], in_=b_value.partition_broadcast(P))
+        load_query_and_key(1)
+        load_w(1)
+        load_query_and_key(2)
+        load_w(2)
+        load_query_and_key(3)
+
+        ident_bf = const.tile([P, P], BF16)
+        make_identity(nc, ident_bf[:])
+        ident_f32 = const.tile([P, P], F32)
+        make_identity(nc, ident_f32[:])
+
+        mask_t = const.tile([P, BLOCKS, SEQ], BF16)
+        for half in range(2):
+            mask_ps = transpose_bank([P, 2, BLOCKS, P])
+            for x in range(2):
+                kb = 2 * half + x
+                for ib in range(BLOCKS):
+                    nc.tensor.transpose(
+                        mask_ps[:, x, ib, :], mask_sb[:, ib, kb * P : (kb + 1) * P], ident_bf[:]
+                    )
+            nc.scalar.copy(
+                out=mask_t[:, 2 * half : 2 * half + 2, :],
+                in_=mask_ps[:].rearrange("p x ib m -> p x (ib m)"),
+            )
+        alibi_ps = transpose_bank([P, P])
+        nc.tensor.transpose(alibi_ps[:], alibi_sb[:], ident_bf[:])
+        alibi_col = const.tile([P, HEADS * BLOCKS], F32)
+        nc.vector.tensor_copy(out=alibi_col[:], in_=alibi_ps[:, 0 : HEADS * BLOCKS])
+
+        hs_codes = const.tile([P, PASSES, BLOCKS, P], U32, align_bytes=64)
+        hs_scales = const.tile([P, PASSES, BLOCKS, P], U8, align_bytes=64)
+
+        def quantise_hidden_states():
+            hs_grouped = const.tile([P, PASSES, BLOCKS, P, 2], F32, align_bytes=64)
+            for t in range(BLOCKS):
+                hs_words = hs_sb[:, t, :].bitcast(F32)
+                for half in range(PASSES // 2):
+                    hs_ps = score_bank([P, 2, 2, P])
+                    for x in range(2):
+                        for u in range(2):
+                            first = (2 * half + x) * (K_PASS // 2) + u * P
+                            nc.tensor.transpose(
+                                hs_ps[:, x, u, :], hs_words[:, first : first + P], ident_f32[:]
+                            )
+                    dst = hs_grouped[:, 2 * half : 2 * half + 2, t, :, :]
+                    src = hs_ps[:].rearrange("p x u m -> p x m u")
+                    if half == 0:
+                        nc.scalar.copy(out=dst, in_=src)
+                    else:
+                        nc.vector.tensor_copy(out=dst, in_=src)
+            for g in range(PASSES):
+                nc.vector.quantize_mx(
+                    out=hs_codes[:, g].rearrange("p t m -> p (t m)").bitcast(FP8X4),
+                    scales=hs_scales[:, g].rearrange("p t m -> p (t m)"),
+                    in_=hs_grouped[:, g].rearrange("p t m u -> p (t m u)").bitcast(BF16),
+                )
+
+        x_of, qk_t_of, e_of, shift_of, row_sum_of = {}, {}, {}, {}, {}
+        e_ps_of, e_grouped_of, e_mx_of = {}, {}, {}
+        w_grouped_of, w_mx_of, v_ps_of, v_grouped_of, v_mx_of = {}, {}, {}, {}, {}
+        out_of = {}
+
+        def added_terms(h):
+            x_sb = work.tile([P, BLOCKS, SEQ], F32, name="x_sb", tag="x_sb")
+            for kb in range(BLOCKS):
+                col = h * BLOCKS + kb
+                nc.gpsimd.tensor_scalar(
+                    out=x_sb[:, kb, :],
+                    in0=mask_t[:, kb, :],
+                    scalar1=alibi_col[:, col : col + 1],
+                    scalar2=INV_SCALE,
+                    op0=ALU.add,
+                    op1=ALU.mult,
+                )
+            x_of[h] = x_sb
+
+        def transpose_query_and_key(h):
+            qk_ps = transpose_bank([P, 2 * BLOCKS, P])
+            for ib in range(BLOCKS):
+                nc.tensor.transpose(
+                    qk_ps[:, ib, :], q_sb[:, h, ib * HEAD_DIM : (ib + 1) * HEAD_DIM], ident_bf[:]
+                )
+            for kb in range(BLOCKS):
+                nc.tensor.transpose(qk_ps[:, BLOCKS + kb, :], k_sb[:, h * BLOCKS + kb, :], ident_bf[:])
+            qk_t = work.tile([P, 2 * BLOCKS, P], BF16, name="qk_t", tag="qk_t")
+            nc.scalar.copy(out=qk_t[:], in_=qk_ps[:])
+            qk_t_of[h] = qk_t
+
+        def start_scores(h):
+            e_of[h] = work.tile([P, BLOCKS, SEQ], BF16, name="e_sb", tag="e_sb")
+            shift_of[h] = (
+                stats.tile([P, BLOCKS], F32, name="neg_max", tag="neg_max"),
+                stats.tile([P, BLOCKS], F32, name="shift", tag="shift"),
+            )
+            row_sum_of[h] = stats.tile([P, BLOCKS], F32, name="row_sum", tag="row_sum")
+
+        def exp_of_scores(h, ib):
+            qk_t, x_sb = qk_t_of[h], x_of[h]
+            neg_max, shift = shift_of[h]
+            one = slice(ib, ib + 1)
+            s_ps = score_bank([P, SEQ])
+            nc.tensor.matmul(
+                out=s_ps[:],
+                lhsT=qk_t[:, ib, :],
+                rhs=qk_t[:, BLOCKS:, :].rearrange("d kb p -> d (kb p)"),
+                start=True,
+                stop=False,
+            )
+            for kb in range(BLOCKS):
+                nc.tensor.matmul(
+                    out=s_ps[:, kb * P : (kb + 1) * P],
+                    lhsT=x_sb[:, kb, ib * P : (ib + 1) * P],
+                    rhs=ident_f32[:],
+                    is_transpose=True,
+                    start=False,
+                    stop=(kb == BLOCKS - 1),
+                )
+            nc.vector.tensor_reduce(out=neg_max[:, one], in_=s_ps[:], axis=AXIS_X, op=ALU.max, negate=True)
+            nc.vector.tensor_scalar_mul(out=shift[:, one], in0=neg_max[:, one], scalar1=SCALE)
+            nc.scalar.activation(
+                out=e_of[h][:, ib, :],
+                in_=s_ps[:],
+                func=ACT.Exp,
+                bias=shift[:, one],
+                scale=SCALE,
+                accum_out=row_sum_of[h][:, one],
+            )
+
+        def transpose_e(h, half):
+            e_ps = transpose_bank([P, 2, BLOCKS, P])
+            for x in range(2):
+                for t in range(BLOCKS):
+                    nc.tensor.transpose(
+                        e_ps[:, x, t, :], e_of[h][:, 2 * half + x, t * P : (t + 1) * P], ident_bf[:]
+                    )
+            e_ps_of[(h, half)] = e_ps
+
+        def group_e(h, half):
+            if half == 0:
+                e_grouped_of[h] = work.tile(
+                    [P, BLOCKS, P, PACK], BF16, name="e_grouped", tag="e_grouped", align_bytes=64
+                )
+            nc.scalar.copy(
+                out=e_grouped_of[h][:, 2 * half : 2 * half + 2, :, :],
+                in_=e_ps_of[(h, half)][:].rearrange("p x t m -> p x m t"),
+            )
+
+        def quantise_e(h):
+            e_codes = work.tile([P, SEQ], U32, name="e_codes", tag="e_codes", align_bytes=64)
+            e_scales = work.tile([P, SEQ], U8, name="e_scales", tag="e_scales", align_bytes=64)
+            nc.vector.quantize_mx(
+                out=e_codes[:].bitcast(FP8X4),
+                scales=e_scales[:],
+                in_=e_grouped_of[h][:].rearrange("p ib m t -> p (ib m t)"),
+            )
+            e_mx_of[h] = (e_codes, e_scales)
+
+        def group_w(h):
+            w_grouped = work.tile([P, PASSES, HEAD_DIM, PACK], BF16, name="w_grouped", tag="w_grouped", align_bytes=64)
+            nc.vector.tensor_copy(
+                out=w_grouped[:].rearrange("p g (c i) t -> p g c t i", i=4),
+                in_=w_raw_of[h // GROUP][:, :, :, head_cols(h)].rearrange("p g t (c i) -> p g c t i", i=4),
+            )
+            w_grouped_of[h] = w_grouped
+
+        def quantise_w(h):
+            w_codes = weights.tile([P, PASSES, HEAD_DIM], U32, name="w_codes", tag="w_codes", align_bytes=64)
+            w_scales = weights.tile([P, PASSES, HEAD_DIM], U8, name="w_scales", tag="w_scales", align_bytes=64)
+            nc.vector.quantize_mx(
+                out=w_codes[:].rearrange("p g n -> p (g n)").bitcast(FP8X4),
+                scales=w_scales[:].rearrange("p g n -> p (g n)"),
+                in_=w_grouped_of[h][:].rearrange("p g n t -> p (g n t)"),
+            )
+            w_mx_of[h] = (w_codes, w_scales)
+
+        def project_value(h):
+            w_codes, w_scales = w_mx_of[h]
+            v_ps = psum.tile([P, BLOCKS, HEAD_DIM], F32, name="v_ps", tag="v_ps")
+            for t in range(BLOCKS):
+                for g in range(PASSES):
+                    nc.tensor.matmul_mx(
+                        out=v_ps[:, t, :],
+                        lhsT=hs_codes[:, g, t, :].bitcast(FP8X4),
+                        lhsT_scale=hs_scales[:, g, t, :],
+                        rhs=w_codes[:, g, :].bitcast(FP8X4),
+                        rhs_scale=w_scales[:, g, :],
+                        start=(g == 0),
+                        stop=(g == PASSES - 1),
+                    )
+            v_ps_of[h] = v_ps
+
+        def group_value(h):
+            v_grouped = work.tile([P, HEAD_DIM, PACK], BF16, name="v_grouped", tag="v_grouped", align_bytes=64)
+            bias = bias_sb[:, h * HEAD_DIM : (h + 1) * HEAD_DIM].unsqueeze(2).to_broadcast([P, HEAD_DIM, PACK])
+            nc.vector.tensor_tensor(
+                out=v_grouped[:], in0=v_ps_of[h][:].rearrange("p t d -> p d t"), in1=bias, op=ALU.add
+            )
+            v_grouped_of[h] = v_grouped
+
+        def quantise_value(h):
+            v_codes = work.tile([P, HEAD_DIM], U32, name="v_codes", tag="v_codes", align_bytes=64)
+            v_scales = work.tile([P, HEAD_DIM], U8, name="v_scales", tag="v_scales", align_bytes=64)
+            nc.vector.quantize_mx(
+                out=v_codes[:].bitcast(FP8X4),
+                scales=v_scales[:],
+                in_=v_grouped_of[h][:].rearrange("p d t -> p (d t)"),
+            )
+            v_mx_of[h] = (v_codes, v_scales)
+
+        def context(h):
+            e_codes, e_scales = e_mx_of[h]
+            v_codes, v_scales = v_mx_of[h]
+            group = h // GROUP
+            if h % GROUP == 0:
+                out_of[group] = work.tile([P, BLOCKS, GROUP_COLS], F32, name="out_sb", tag="out_sb")
+            ctx_ps = psum.tile([P, BLOCKS, HEAD_DIM], F32, name="ctx_ps", tag="ctx_ps")
+            for ib in range(BLOCKS):
+                queries = slice(ib * P, (ib + 1) * P)
+                nc.tensor.matmul_mx(
+                    out=ctx_ps[:, ib, :],
+                    lhsT=e_codes[:, queries].bitcast(FP8X4),
+                    lhsT_scale=e_scales[:, queries],
+                    rhs=v_codes[:].bitcast(FP8X4),
+                    rhs_scale=v_scales[:],
+                    start=True,
+                    stop=True,
+                )
+            inv_sum = stats.tile([P, BLOCKS], F32, name="inv_sum", tag="inv_sum")
+            nc.vector.reciprocal(out=inv_sum[:], in_=row_sum_of[h][:])
+            nc.vector.tensor_tensor(
+                out=out_of[group][:, :, head_cols(h)],
+                in0=ctx_ps[:],
+                in1=inv_sum[:].unsqueeze(2).to_broadcast([P, BLOCKS, HEAD_DIM]),
+                op=ALU.mult,
+            )
+            if h % GROUP == GROUP - 1:
+                cols = slice(group * GROUP_COLS, (group + 1) * GROUP_COLS)
+                nc.sync.dma_start(out=out_rows[:, :, cols], in_=out_of[group][:])
+
+        def is_head(h):
+            return 0 <= h < HEADS
+
+        added_terms(0)
+        transpose_query_and_key(0)
+        for step in range(HEADS + LAG_CONTEXT):
+            h_scores = step
+            h_transpose = step - LAG_TRANSPOSE
+            h_value = step - LAG_VALUE
+            h_context = step - LAG_CONTEXT
+
+            if is_head(h_value):
+                quantise_e(h_value)
+            if is_head(h_scores + 1):
+                added_terms(h_scores + 1)
+            if is_head(h_scores):
+                start_scores(h_scores)
+                exp_of_scores(h_scores, 0)
+                exp_of_scores(h_scores, 1)
+            if is_head(h_transpose):
+                transpose_e(h_transpose, 0)
+                group_e(h_transpose, 0)
+                group_w(h_transpose)
+                if h_transpose % GROUP == GROUP - 1 and h_transpose // GROUP + 3 < GROUPS:
+                    load_w(h_transpose // GROUP + 3)
+            if is_head(h_scores):
+                exp_of_scores(h_scores, 2)
+            if is_head(h_transpose):
+                transpose_e(h_transpose, 1)
+            if is_head(h_scores):
+                exp_of_scores(h_scores, 3)
+            if is_head(h_scores + 1):
+                transpose_query_and_key(h_scores + 1)
+            if is_head(h_transpose):
+                group_e(h_transpose, 1)
+            if step == HIDDEN_STATES_STEP:
+                quantise_hidden_states()
+            if is_head(h_context):
+                context(h_context)
+            if is_head(h_value):
+                project_value(h_value)
+                group_value(h_value)
+            if is_head(h_transpose):
+                quantise_w(h_transpose)
+            if is_head(h_value):
+                quantise_value(h_value)

@@ -30,9 +30,7 @@ GROUP_COLS = GROUP * HEAD_DIM
 SCALE = 1.0 / math.sqrt(HEAD_DIM)
 INV_SCALE = math.sqrt(HEAD_DIM)
 
-LAG_TRANSPOSE = 1
-LAG_VALUE = 2
-LAG_CONTEXT = 3
+DRAIN_STEPS = 3
 HIDDEN_STATES_STEP = 1
 
 FLOPS = 2 * SEQ * HIDDEN * HIDDEN + 2 * (2 * HEADS * SEQ * SEQ * HEAD_DIM)
@@ -55,14 +53,15 @@ def tile_fastbloomattention_pa_kernel(
         const = stack.enter_context(tc.tile_pool(name="const", bufs=1))
         weights = stack.enter_context(tc.tile_pool(name="weights", bufs=3))
         work = stack.enter_context(tc.tile_pool(name="work", bufs=2))
-        stats = stack.enter_context(tc.tile_pool(name="stats", bufs=LAG_CONTEXT + 1))
+        stats = stack.enter_context(tc.tile_pool(name="stats", bufs=DRAIN_STEPS + 1))
         psum = stack.enter_context(tc.psum_pool(name="psum", bufs=1))
+        stack.enter_context(tc.manual_schedule())
 
         def score_bank(shape):
-            return psum.tile(shape, F32, name="score_bank", tag="score_bank", bufs=3)
+            return psum.tile(shape, F32, name="score_bank", tag="score_bank", bufs=4)
 
         def transpose_bank(shape):
-            return psum.tile(shape, BF16, name="transpose_bank", tag="transpose_bank", bufs=3)
+            return psum.tile(shape, BF16, name="transpose_bank", tag="transpose_bank", bufs=2)
 
         def head_cols(h):
             return slice((h % GROUP) * HEAD_DIM, (h % GROUP + 1) * HEAD_DIM)
@@ -97,7 +96,8 @@ def tile_fastbloomattention_pa_kernel(
         load_query_and_key(0)
         load_w(0)
         hs_sb = const.tile([P, BLOCKS, HIDDEN], BF16)
-        nc.sync.dma_start(out=hs_sb[:], in_=hs_rows)
+        for t in range(BLOCKS):
+            nc.sync.dma_start(out=hs_sb[:, t, :], in_=hs_rows[:, t, :])
         bias_sb = const.tile([P, HIDDEN], BF16)
         nc.sync.dma_start(out=bias_sb[:], in_=b_value.partition_broadcast(P))
         load_query_and_key(1)
@@ -129,38 +129,34 @@ def tile_fastbloomattention_pa_kernel(
         alibi_col = const.tile([P, HEADS * BLOCKS], F32)
         nc.vector.tensor_copy(out=alibi_col[:], in_=alibi_ps[:, 0 : HEADS * BLOCKS])
 
-        hs_codes = const.tile([P, PASSES, BLOCKS, P], U32, align_bytes=64)
-        hs_scales = const.tile([P, PASSES, BLOCKS, P], U8, align_bytes=64)
+        hs_grouped = const.tile([P, BLOCKS, PASSES, P, 2], F32, align_bytes=64)
+        hs_codes = const.tile([P, BLOCKS, PASSES, P], U32, align_bytes=64)
+        hs_scales = const.tile([P, BLOCKS, PASSES, P], U8, align_bytes=64)
 
-        def quantise_hidden_states():
-            hs_grouped = const.tile([P, PASSES, BLOCKS, P, 2], F32, align_bytes=64)
-            for t in range(BLOCKS):
-                hs_words = hs_sb[:, t, :].bitcast(F32)
-                for half in range(PASSES // 2):
-                    hs_ps = score_bank([P, 2, 2, P])
-                    for x in range(2):
-                        for u in range(2):
-                            first = (2 * half + x) * (K_PASS // 2) + u * P
-                            nc.tensor.transpose(
-                                hs_ps[:, x, u, :], hs_words[:, first : first + P], ident_f32[:]
-                            )
-                    dst = hs_grouped[:, 2 * half : 2 * half + 2, t, :, :]
-                    src = hs_ps[:].rearrange("p x u m -> p x m u")
-                    if half == 0:
-                        nc.scalar.copy(out=dst, in_=src)
-                    else:
-                        nc.vector.tensor_copy(out=dst, in_=src)
-            for g in range(PASSES):
-                nc.vector.quantize_mx(
-                    out=hs_codes[:, g].rearrange("p t m -> p (t m)").bitcast(FP8X4),
-                    scales=hs_scales[:, g].rearrange("p t m -> p (t m)"),
-                    in_=hs_grouped[:, g].rearrange("p t m u -> p (t m u)").bitcast(BF16),
-                )
+        def quantise_hidden_states(t):
+            hs_words = hs_sb[:, t, :].bitcast(F32)
+            for half in range(PASSES // 2):
+                hs_ps = score_bank([P, 2, 2, P])
+                for x in range(2):
+                    for u in range(2):
+                        first = (2 * half + x) * (K_PASS // 2) + u * P
+                        nc.tensor.transpose(hs_ps[:, x, u, :], hs_words[:, first : first + P], ident_f32[:])
+                dst = hs_grouped[:, t, 2 * half : 2 * half + 2, :, :]
+                src = hs_ps[:].rearrange("p x u m -> p x m u")
+                if half == 0:
+                    nc.scalar.copy(out=dst, in_=src)
+                else:
+                    nc.vector.tensor_copy(out=dst, in_=src)
+            nc.vector.quantize_mx(
+                out=hs_codes[:, t].rearrange("p g m -> p (g m)").bitcast(FP8X4),
+                scales=hs_scales[:, t].rearrange("p g m -> p (g m)"),
+                in_=hs_grouped[:, t].rearrange("p g m u -> p (g m u)").bitcast(BF16),
+            )
 
-        x_of, qk_t_of, e_of, shift_of, row_sum_of = {}, {}, {}, {}, {}
+        x_of, qk_ps_of, qk_t_of, s_ps_of, e_of, shift_of, row_sum_of = {}, {}, {}, {}, {}, {}, {}
         e_ps_of, e_grouped_of, e_mx_of = {}, {}, {}
         w_grouped_of, w_mx_of, v_ps_of, v_grouped_of, v_mx_of = {}, {}, {}, {}, {}
-        out_of = {}
+        ctx_ps_of, out_of = {}, {}
 
         def added_terms(h):
             x_sb = work.tile([P, BLOCKS, SEQ], F32, name="x_sb", tag="x_sb")
@@ -184,22 +180,22 @@ def tile_fastbloomattention_pa_kernel(
                 )
             for kb in range(BLOCKS):
                 nc.tensor.transpose(qk_ps[:, BLOCKS + kb, :], k_sb[:, h * BLOCKS + kb, :], ident_bf[:])
+            qk_ps_of[h] = qk_ps
+
+        def copy_query_and_key(h):
             qk_t = work.tile([P, 2 * BLOCKS, P], BF16, name="qk_t", tag="qk_t")
-            nc.scalar.copy(out=qk_t[:], in_=qk_ps[:])
+            nc.scalar.copy(out=qk_t[:], in_=qk_ps_of[h][:])
             qk_t_of[h] = qk_t
 
-        def start_scores(h):
-            e_of[h] = work.tile([P, BLOCKS, SEQ], BF16, name="e_sb", tag="e_sb")
-            shift_of[h] = (
-                stats.tile([P, BLOCKS], F32, name="neg_max", tag="neg_max"),
-                stats.tile([P, BLOCKS], F32, name="shift", tag="shift"),
-            )
-            row_sum_of[h] = stats.tile([P, BLOCKS], F32, name="row_sum", tag="row_sum")
-
-        def exp_of_scores(h, ib):
+        def score_matmul(h, ib):
+            if ib == 0:
+                e_of[h] = work.tile([P, BLOCKS, SEQ], BF16, name="e_sb", tag="e_sb")
+                shift_of[h] = (
+                    stats.tile([P, BLOCKS], F32, name="neg_max", tag="neg_max"),
+                    stats.tile([P, BLOCKS], F32, name="shift", tag="shift"),
+                )
+                row_sum_of[h] = stats.tile([P, BLOCKS], F32, name="row_sum", tag="row_sum")
             qk_t, x_sb = qk_t_of[h], x_of[h]
-            neg_max, shift = shift_of[h]
-            one = slice(ib, ib + 1)
             s_ps = score_bank([P, SEQ])
             nc.tensor.matmul(
                 out=s_ps[:],
@@ -217,13 +213,23 @@ def tile_fastbloomattention_pa_kernel(
                     start=False,
                     stop=(kb == BLOCKS - 1),
                 )
-            nc.vector.tensor_reduce(out=neg_max[:, one], in_=s_ps[:], axis=AXIS_X, op=ALU.max, negate=True)
+            s_ps_of[(h, ib)] = s_ps
+
+        def row_max(h, ib):
+            neg_max, shift = shift_of[h]
+            one = slice(ib, ib + 1)
+            nc.vector.tensor_reduce(
+                out=neg_max[:, one], in_=s_ps_of[(h, ib)][:], axis=AXIS_X, op=ALU.max, negate=True
+            )
             nc.vector.tensor_scalar_mul(out=shift[:, one], in0=neg_max[:, one], scalar1=SCALE)
+
+        def exponential(h, ib):
+            one = slice(ib, ib + 1)
             nc.scalar.activation(
                 out=e_of[h][:, ib, :],
-                in_=s_ps[:],
+                in_=s_ps_of[(h, ib)][:],
                 func=ACT.Exp,
-                bias=shift[:, one],
+                bias=shift_of[h][1][:, one],
                 scale=SCALE,
                 accum_out=row_sum_of[h][:, one],
             )
@@ -264,10 +270,12 @@ def tile_fastbloomattention_pa_kernel(
                 in_=w_raw_of[h // GROUP][:, :, :, head_cols(h)].rearrange("p g t (c i) -> p g c t i", i=4),
             )
             w_grouped_of[h] = w_grouped
+            if h % GROUP == GROUP - 1 and h // GROUP + 3 < GROUPS:
+                load_w(h // GROUP + 3)
 
         def quantise_w(h):
-            w_codes = weights.tile([P, PASSES, HEAD_DIM], U32, name="w_codes", tag="w_codes", align_bytes=64)
-            w_scales = weights.tile([P, PASSES, HEAD_DIM], U8, name="w_scales", tag="w_scales", align_bytes=64)
+            w_codes = work.tile([P, PASSES, HEAD_DIM], U32, name="w_codes", tag="w_codes", align_bytes=64)
+            w_scales = work.tile([P, PASSES, HEAD_DIM], U8, name="w_scales", tag="w_scales", align_bytes=64)
             nc.vector.quantize_mx(
                 out=w_codes[:].rearrange("p g n -> p (g n)").bitcast(FP8X4),
                 scales=w_scales[:].rearrange("p g n -> p (g n)"),
@@ -282,8 +290,8 @@ def tile_fastbloomattention_pa_kernel(
                 for g in range(PASSES):
                     nc.tensor.matmul_mx(
                         out=v_ps[:, t, :],
-                        lhsT=hs_codes[:, g, t, :].bitcast(FP8X4),
-                        lhsT_scale=hs_scales[:, g, t, :],
+                        lhsT=hs_codes[:, t, g, :].bitcast(FP8X4),
+                        lhsT_scale=hs_scales[:, t, g, :],
                         rhs=w_codes[:, g, :].bitcast(FP8X4),
                         rhs_scale=w_scales[:, g, :],
                         start=(g == 0),
@@ -312,9 +320,6 @@ def tile_fastbloomattention_pa_kernel(
         def context(h):
             e_codes, e_scales = e_mx_of[h]
             v_codes, v_scales = v_mx_of[h]
-            group = h // GROUP
-            if h % GROUP == 0:
-                out_of[group] = work.tile([P, BLOCKS, GROUP_COLS], F32, name="out_sb", tag="out_sb")
             ctx_ps = psum.tile([P, BLOCKS, HEAD_DIM], F32, name="ctx_ps", tag="ctx_ps")
             for ib in range(BLOCKS):
                 queries = slice(ib * P, (ib + 1) * P)
@@ -327,11 +332,17 @@ def tile_fastbloomattention_pa_kernel(
                     start=True,
                     stop=True,
                 )
+            ctx_ps_of[h] = ctx_ps
+
+        def divide(h):
+            group = h // GROUP
+            if h % GROUP == 0:
+                out_of[group] = work.tile([P, BLOCKS, GROUP_COLS], F32, name="out_sb", tag="out_sb")
             inv_sum = stats.tile([P, BLOCKS], F32, name="inv_sum", tag="inv_sum")
             nc.vector.reciprocal(out=inv_sum[:], in_=row_sum_of[h][:])
             nc.vector.tensor_tensor(
                 out=out_of[group][:, :, head_cols(h)],
-                in0=ctx_ps[:],
+                in0=ctx_ps_of[h][:],
                 in1=inv_sum[:].unsqueeze(2).to_broadcast([P, BLOCKS, HEAD_DIM]),
                 op=ALU.mult,
             )
@@ -339,49 +350,50 @@ def tile_fastbloomattention_pa_kernel(
                 cols = slice(group * GROUP_COLS, (group + 1) * GROUP_COLS)
                 nc.sync.dma_start(out=out_rows[:, :, cols], in_=out_of[group][:])
 
-        def is_head(h):
-            return 0 <= h < HEADS
+        def on_head(piece, h, *args):
+            if 0 <= h < HEADS:
+                piece(h, *args)
+
+        def on_hidden_states(step, t):
+            if step == HIDDEN_STATES_STEP:
+                quantise_hidden_states(t)
 
         added_terms(0)
         transpose_query_and_key(0)
-        for step in range(HEADS + LAG_CONTEXT):
-            h_scores = step
-            h_transpose = step - LAG_TRANSPOSE
-            h_value = step - LAG_VALUE
-            h_context = step - LAG_CONTEXT
+        copy_query_and_key(0)
+        for h in range(HEADS + DRAIN_STEPS):
+            on_head(added_terms, h + 1)
 
-            if is_head(h_value):
-                quantise_e(h_value)
-            if is_head(h_scores + 1):
-                added_terms(h_scores + 1)
-            if is_head(h_scores):
-                start_scores(h_scores)
-                exp_of_scores(h_scores, 0)
-                exp_of_scores(h_scores, 1)
-            if is_head(h_transpose):
-                transpose_e(h_transpose, 0)
-                group_e(h_transpose, 0)
-                group_w(h_transpose)
-                if h_transpose % GROUP == GROUP - 1 and h_transpose // GROUP + 3 < GROUPS:
-                    load_w(h_transpose // GROUP + 3)
-            if is_head(h_scores):
-                exp_of_scores(h_scores, 2)
-            if is_head(h_transpose):
-                transpose_e(h_transpose, 1)
-            if is_head(h_scores):
-                exp_of_scores(h_scores, 3)
-            if is_head(h_scores + 1):
-                transpose_query_and_key(h_scores + 1)
-            if is_head(h_transpose):
-                group_e(h_transpose, 1)
-            if step == HIDDEN_STATES_STEP:
-                quantise_hidden_states()
-            if is_head(h_context):
-                context(h_context)
-            if is_head(h_value):
-                project_value(h_value)
-                group_value(h_value)
-            if is_head(h_transpose):
-                quantise_w(h_transpose)
-            if is_head(h_value):
-                quantise_value(h_value)
+            on_head(score_matmul, h, 0)
+            on_head(transpose_e, h - 1, 0)
+            on_head(row_max, h - 1, 3)
+            on_head(quantise_e, h - 2)
+            on_head(exponential, h - 1, 2)
+            on_hidden_states(h, 0)
+
+            on_head(score_matmul, h, 1)
+            on_head(transpose_query_and_key, h + 1)
+            on_head(row_max, h, 0)
+            on_head(group_value, h - 2)
+            on_head(quantise_w, h - 1)
+            on_head(exponential, h - 1, 3)
+            on_head(group_e, h - 1, 0)
+            on_hidden_states(h, 1)
+
+            on_head(score_matmul, h, 2)
+            on_head(transpose_e, h - 1, 1)
+            on_head(row_max, h, 1)
+            on_head(quantise_value, h - 2)
+            on_head(divide, h - 3)
+            on_head(exponential, h, 0)
+            on_head(copy_query_and_key, h + 1)
+            on_hidden_states(h, 2)
+
+            on_head(score_matmul, h, 3)
+            on_hidden_states(h, 3)
+            on_head(context, h - 2)
+            on_head(project_value, h - 1)
+            on_head(row_max, h, 2)
+            on_head(group_w, h)
+            on_head(exponential, h, 1)
+            on_head(group_e, h - 1, 1)

@@ -11,7 +11,6 @@ U32 = mybir.dt.uint32
 FP8X4 = mybir.dt.float8_e4m3fn_x4
 ALU = mybir.AluOpType
 ACT = mybir.ActivationFunctionType
-AXIS_X = mybir.AxisListType.X
 
 P = 128
 PACK = 4
@@ -190,10 +189,7 @@ def tile_fastbloomattention_pa_kernel(
         def score_matmul(h, ib):
             if ib == 0:
                 e_of[h] = work.tile([P, BLOCKS, SEQ], BF16, name="e_sb", tag="e_sb")
-                shift_of[h] = (
-                    stats.tile([P, BLOCKS], F32, name="neg_max", tag="neg_max"),
-                    stats.tile([P, BLOCKS], F32, name="shift", tag="shift"),
-                )
+                shift_of[h] = stats.tile([P, BLOCKS], F32, name="shift", tag="shift")
                 row_sum_of[h] = stats.tile([P, BLOCKS], F32, name="row_sum", tag="row_sum")
             qk_t, x_sb = qk_t_of[h], x_of[h]
             s_ps = score_bank([P, SEQ])
@@ -216,12 +212,16 @@ def tile_fastbloomattention_pa_kernel(
             s_ps_of[(h, ib)] = s_ps
 
         def row_max(h, ib):
-            neg_max, shift = shift_of[h]
-            one = slice(ib, ib + 1)
-            nc.vector.tensor_reduce(
-                out=neg_max[:, one], in_=s_ps_of[(h, ib)][:], axis=AXIS_X, op=ALU.max, negate=True
+            products = work.tile([P, SEQ], F32, name="products", tag="products")
+            nc.vector.tensor_scalar(
+                out=products[:],
+                in0=s_ps_of[(h, ib)][:],
+                scalar1=-SCALE,
+                scalar2=None,
+                op0=ALU.mult,
+                op1=ALU.min,
+                accum_out=shift_of[h][:, ib : ib + 1],
             )
-            nc.vector.tensor_scalar_mul(out=shift[:, one], in0=neg_max[:, one], scalar1=SCALE)
 
         def exponential(h, ib):
             one = slice(ib, ib + 1)
@@ -229,7 +229,7 @@ def tile_fastbloomattention_pa_kernel(
                 out=e_of[h][:, ib, :],
                 in_=s_ps_of[(h, ib)][:],
                 func=ACT.Exp,
-                bias=shift_of[h][1][:, one],
+                bias=shift_of[h][:, one],
                 scale=SCALE,
                 accum_out=row_sum_of[h][:, one],
             )
@@ -367,7 +367,7 @@ def tile_fastbloomattention_pa_kernel(
             on_head(score_matmul, h, 0)
             on_head(transpose_e, h - 1, 0)
             on_head(row_max, h - 1, 3)
-            on_head(quantise_e, h - 2)
+            on_head(divide, h - 3)
             on_head(exponential, h - 1, 2)
             on_hidden_states(h, 0)
 
@@ -375,7 +375,6 @@ def tile_fastbloomattention_pa_kernel(
             on_head(transpose_query_and_key, h + 1)
             on_head(row_max, h, 0)
             on_head(group_value, h - 2)
-            on_head(quantise_w, h - 1)
             on_head(exponential, h - 1, 3)
             on_head(group_e, h - 1, 0)
             on_hidden_states(h, 1)
@@ -384,7 +383,8 @@ def tile_fastbloomattention_pa_kernel(
             on_head(transpose_e, h - 1, 1)
             on_head(row_max, h, 1)
             on_head(quantise_value, h - 2)
-            on_head(divide, h - 3)
+            on_head(quantise_e, h - 2)
+            on_head(quantise_w, h - 1)
             on_head(exponential, h, 0)
             on_head(copy_query_and_key, h + 1)
             on_hidden_states(h, 2)
@@ -393,7 +393,7 @@ def tile_fastbloomattention_pa_kernel(
             on_hidden_states(h, 3)
             on_head(context, h - 2)
             on_head(project_value, h - 1)
-            on_head(row_max, h, 2)
             on_head(group_w, h)
+            on_head(row_max, h, 2)
             on_head(exponential, h, 1)
             on_head(group_e, h - 1, 1)

@@ -30,7 +30,7 @@ SCALE = 1.0 / math.sqrt(HEAD_DIM)
 INV_SCALE = math.sqrt(HEAD_DIM)
 
 DRAIN_STEPS = 3
-HIDDEN_STATES_STEP = 1
+W_BUFFERS = 3
 
 FLOPS = 2 * SEQ * HIDDEN * HIDDEN + 2 * (2 * HEADS * SEQ * SEQ * HEAD_DIM)
 
@@ -50,7 +50,7 @@ def tile_fastbloomattention_pa_kernel(
 
     with ExitStack() as stack:
         const = stack.enter_context(tc.tile_pool(name="const", bufs=1))
-        weights = stack.enter_context(tc.tile_pool(name="weights", bufs=3))
+        weights = stack.enter_context(tc.tile_pool(name="weights", bufs=W_BUFFERS))
         work = stack.enter_context(tc.tile_pool(name="work", bufs=2))
         stats = stack.enter_context(tc.tile_pool(name="stats", bufs=DRAIN_STEPS + 1))
         psum = stack.enter_context(tc.psum_pool(name="psum", bufs=1))
@@ -74,10 +74,9 @@ def tile_fastbloomattention_pa_kernel(
         q_sb = const.tile([P, HEADS, BLOCKS * HEAD_DIM], BF16)
         k_sb = const.tile([P, HEADS * BLOCKS, HEAD_DIM], BF16)
 
-        def load_query_and_key(group):
-            heads = slice(group * GROUP, (group + 1) * GROUP)
-            blocks = slice(group * GROUP * BLOCKS, (group + 1) * GROUP * BLOCKS)
-            nc.sync.dma_start(out=q_sb[:, heads, :], in_=q_rows[:, heads, :])
+        def load_query_and_key(first, stop):
+            nc.sync.dma_start(out=q_sb[:, first:stop, :], in_=q_rows[:, first:stop, :])
+            blocks = slice(first * BLOCKS, stop * BLOCKS)
             nc.sync.dma_start(out=k_sb[:, blocks, :], in_=k_rows[:, blocks, :])
 
         w_raw_of = {}
@@ -92,18 +91,18 @@ def tile_fastbloomattention_pa_kernel(
                     )
             w_raw_of[group] = w_raw
 
-        load_query_and_key(0)
-        load_w(0)
         hs_sb = const.tile([P, BLOCKS, HIDDEN], BF16)
         for t in range(BLOCKS):
             nc.sync.dma_start(out=hs_sb[:, t, :], in_=hs_rows[:, t, :])
+        load_query_and_key(0, 1)
+        load_query_and_key(1, GROUP)
+        load_w(0)
         bias_sb = const.tile([P, HIDDEN], BF16)
         nc.sync.dma_start(out=bias_sb[:], in_=b_value.partition_broadcast(P))
-        load_query_and_key(1)
-        load_w(1)
-        load_query_and_key(2)
-        load_w(2)
-        load_query_and_key(3)
+        for group in range(1, GROUPS):
+            load_query_and_key(group * GROUP, (group + 1) * GROUP)
+            if group < W_BUFFERS:
+                load_w(group)
 
         ident_bf = const.tile([P, P], BF16)
         make_identity(nc, ident_bf[:])
@@ -132,7 +131,9 @@ def tile_fastbloomattention_pa_kernel(
         hs_codes = const.tile([P, BLOCKS, PASSES, P], U32, align_bytes=64)
         hs_scales = const.tile([P, BLOCKS, PASSES, P], U8, align_bytes=64)
 
-        def quantise_hidden_states(t):
+        hs_ps_of = {}
+
+        def transpose_hidden_states(t):
             hs_words = hs_sb[:, t, :].bitcast(F32)
             for half in range(PASSES // 2):
                 hs_ps = score_bank([P, 2, 2, P])
@@ -140,12 +141,15 @@ def tile_fastbloomattention_pa_kernel(
                     for u in range(2):
                         first = (2 * half + x) * (K_PASS // 2) + u * P
                         nc.tensor.transpose(hs_ps[:, x, u, :], hs_words[:, first : first + P], ident_f32[:])
-                dst = hs_grouped[:, t, 2 * half : 2 * half + 2, :, :]
-                src = hs_ps[:].rearrange("p x u m -> p x m u")
-                if half == 0:
-                    nc.scalar.copy(out=dst, in_=src)
-                else:
-                    nc.vector.tensor_copy(out=dst, in_=src)
+                hs_ps_of[(t, half)] = hs_ps
+
+        def group_hidden_states(t):
+            nc.scalar.copy(out=hs_grouped[:, t, 0:2, :, :], in_=hs_ps_of[(t, 0)][:].rearrange("p x u m -> p x m u"))
+            nc.vector.tensor_copy(
+                out=hs_grouped[:, t, 2:4, :, :], in_=hs_ps_of[(t, 1)][:].rearrange("p x u m -> p x m u")
+            )
+
+        def quantise_hidden_states(t):
             nc.vector.quantize_mx(
                 out=hs_codes[:, t].rearrange("p g m -> p (g m)").bitcast(FP8X4),
                 scales=hs_scales[:, t].rearrange("p g m -> p (g m)"),
@@ -155,7 +159,7 @@ def tile_fastbloomattention_pa_kernel(
         x_of, qk_ps_of, qk_t_of, s_ps_of, e_of, shift_of, row_sum_of = {}, {}, {}, {}, {}, {}, {}
         e_ps_of, e_grouped_of, e_mx_of = {}, {}, {}
         w_grouped_of, w_mx_of, v_ps_of, v_grouped_of, v_mx_of = {}, {}, {}, {}, {}
-        ctx_ps_of, out_of = {}, {}
+        ctx_ps_of = {}
 
         def added_terms(h):
             x_sb = work.tile([P, BLOCKS, SEQ], F32, name="x_sb", tag="x_sb")
@@ -270,8 +274,8 @@ def tile_fastbloomattention_pa_kernel(
                 in_=w_raw_of[h // GROUP][:, :, :, head_cols(h)].rearrange("p g t (c i) -> p g c t i", i=4),
             )
             w_grouped_of[h] = w_grouped
-            if h % GROUP == GROUP - 1 and h // GROUP + 3 < GROUPS:
-                load_w(h // GROUP + 3)
+            if h % GROUP == GROUP - 1 and h // GROUP + W_BUFFERS < GROUPS:
+                load_w(h // GROUP + W_BUFFERS)
 
         def quantise_w(h):
             w_codes = work.tile([P, PASSES, HEAD_DIM], U32, name="w_codes", tag="w_codes", align_bytes=64)
@@ -335,32 +339,33 @@ def tile_fastbloomattention_pa_kernel(
             ctx_ps_of[h] = ctx_ps
 
         def divide(h):
-            group = h // GROUP
-            if h % GROUP == 0:
-                out_of[group] = work.tile([P, BLOCKS, GROUP_COLS], F32, name="out_sb", tag="out_sb")
             inv_sum = stats.tile([P, BLOCKS], F32, name="inv_sum", tag="inv_sum")
             nc.vector.reciprocal(out=inv_sum[:], in_=row_sum_of[h][:])
+            out_sb = work.tile([P, BLOCKS, HEAD_DIM], F32, name="out_sb", tag="out_sb")
             nc.vector.tensor_tensor(
-                out=out_of[group][:, :, head_cols(h)],
+                out=out_sb[:],
                 in0=ctx_ps_of[h][:],
                 in1=inv_sum[:].unsqueeze(2).to_broadcast([P, BLOCKS, HEAD_DIM]),
                 op=ALU.mult,
             )
-            if h % GROUP == GROUP - 1:
-                cols = slice(group * GROUP_COLS, (group + 1) * GROUP_COLS)
-                nc.sync.dma_start(out=out_rows[:, :, cols], in_=out_of[group][:])
+            nc.sync.dma_start(out=out_rows[:, :, h * HEAD_DIM : (h + 1) * HEAD_DIM], in_=out_sb[:])
+
+        def on_block(piece, t):
+            if 0 <= t < BLOCKS:
+                piece(t)
 
         def on_head(piece, h, *args):
             if 0 <= h < HEADS:
                 piece(h, *args)
 
-        def on_hidden_states(step, t):
-            if step == HIDDEN_STATES_STEP:
-                quantise_hidden_states(t)
-
         added_terms(0)
+        for t in range(BLOCKS + 2):
+            on_block(transpose_hidden_states, t)
+            on_block(group_hidden_states, t - 1)
+            on_block(quantise_hidden_states, t - 2)
         transpose_query_and_key(0)
         copy_query_and_key(0)
+
         for h in range(HEADS + DRAIN_STEPS):
             on_head(added_terms, h + 1)
 
@@ -368,16 +373,15 @@ def tile_fastbloomattention_pa_kernel(
             on_head(transpose_e, h - 1, 0)
             on_head(row_max, h - 1, 3)
             on_head(divide, h - 3)
+            on_head(group_value, h - 2)
             on_head(exponential, h - 1, 2)
-            on_hidden_states(h, 0)
 
             on_head(score_matmul, h, 1)
             on_head(transpose_query_and_key, h + 1)
             on_head(row_max, h, 0)
-            on_head(group_value, h - 2)
+            on_head(group_w, h - 1)
             on_head(exponential, h - 1, 3)
             on_head(group_e, h - 1, 0)
-            on_hidden_states(h, 1)
 
             on_head(score_matmul, h, 2)
             on_head(transpose_e, h - 1, 1)
@@ -387,13 +391,10 @@ def tile_fastbloomattention_pa_kernel(
             on_head(quantise_w, h - 1)
             on_head(exponential, h, 0)
             on_head(copy_query_and_key, h + 1)
-            on_hidden_states(h, 2)
 
             on_head(score_matmul, h, 3)
-            on_hidden_states(h, 3)
             on_head(context, h - 2)
             on_head(project_value, h - 1)
-            on_head(group_w, h)
             on_head(row_max, h, 2)
             on_head(exponential, h, 1)
             on_head(group_e, h - 1, 1)

@@ -95,10 +95,11 @@ def tile_fastbloomattention_pa_kernel(
         for t in range(BLOCKS):
             nc.sync.dma_start(out=hs_sb[:, t, :], in_=hs_rows[:, t, :])
         load_query_and_key(0, 1)
-        load_query_and_key(1, GROUP)
+        load_query_and_key(1, 2)
         load_w(0)
         bias_sb = const.tile([P, HIDDEN], BF16)
         nc.sync.dma_start(out=bias_sb[:], in_=b_value.partition_broadcast(P))
+        load_query_and_key(2, GROUP)
         for group in range(1, GROUPS):
             load_query_and_key(group * GROUP, (group + 1) * GROUP)
             if group < W_BUFFERS:
@@ -373,28 +374,28 @@ def tile_fastbloomattention_pa_kernel(
             on_head(transpose_e, h - 1, 0)
             on_head(row_max, h - 1, 3)
             on_head(divide, h - 3)
-            on_head(group_value, h - 2)
+            on_head(group_value, h - 1)
             on_head(exponential, h - 1, 2)
 
             on_head(score_matmul, h, 1)
             on_head(transpose_query_and_key, h + 1)
             on_head(row_max, h, 0)
-            on_head(group_w, h - 1)
+            on_head(group_w, h)
             on_head(exponential, h - 1, 3)
             on_head(group_e, h - 1, 0)
 
             on_head(score_matmul, h, 2)
             on_head(transpose_e, h - 1, 1)
             on_head(row_max, h, 1)
-            on_head(quantise_value, h - 2)
+            on_head(quantise_value, h - 1)
             on_head(quantise_e, h - 2)
-            on_head(quantise_w, h - 1)
+            on_head(quantise_w, h)
             on_head(exponential, h, 0)
             on_head(copy_query_and_key, h + 1)
 
             on_head(score_matmul, h, 3)
             on_head(context, h - 2)
-            on_head(project_value, h - 1)
+            on_head(project_value, h)
             on_head(row_max, h, 2)
             on_head(exponential, h, 1)
             on_head(group_e, h - 1, 1)

@@ -95,11 +95,10 @@ def tile_fastbloomattention_pa_kernel(
         for t in range(BLOCKS):
             nc.sync.dma_start(out=hs_sb[:, t, :], in_=hs_rows[:, t, :])
         load_query_and_key(0, 1)
-        load_query_and_key(1, 2)
+        load_query_and_key(1, GROUP)
         load_w(0)
         bias_sb = const.tile([P, HIDDEN], BF16)
         nc.sync.dma_start(out=bias_sb[:], in_=b_value.partition_broadcast(P))
-        load_query_and_key(2, GROUP)
         for group in range(1, GROUPS):
             load_query_and_key(group * GROUP, (group + 1) * GROUP)
             if group < W_BUFFERS:
@@ -198,22 +197,22 @@ def tile_fastbloomattention_pa_kernel(
                 row_sum_of[h] = stats.tile([P, BLOCKS], F32, name="row_sum", tag="row_sum")
             qk_t, x_sb = qk_t_of[h], x_of[h]
             s_ps = score_bank([P, SEQ])
-            nc.tensor.matmul(
-                out=s_ps[:],
-                lhsT=qk_t[:, ib, :],
-                rhs=qk_t[:, BLOCKS:, :].rearrange("d kb p -> d (kb p)"),
-                start=True,
-                stop=False,
-            )
             for kb in range(BLOCKS):
                 nc.tensor.matmul(
                     out=s_ps[:, kb * P : (kb + 1) * P],
                     lhsT=x_sb[:, kb, ib * P : (ib + 1) * P],
                     rhs=ident_f32[:],
                     is_transpose=True,
-                    start=False,
-                    stop=(kb == BLOCKS - 1),
+                    start=(kb == 0),
+                    stop=False,
                 )
+            nc.tensor.matmul(
+                out=s_ps[:],
+                lhsT=qk_t[:, ib, :],
+                rhs=qk_t[:, BLOCKS:, :].rearrange("d kb p -> d (kb p)"),
+                start=False,
+                stop=True,
+            )
             s_ps_of[(h, ib)] = s_ps
 
         def row_max(h, ib):
@@ -374,28 +373,28 @@ def tile_fastbloomattention_pa_kernel(
             on_head(transpose_e, h - 1, 0)
             on_head(row_max, h - 1, 3)
             on_head(divide, h - 3)
-            on_head(group_value, h - 1)
+            on_head(group_value, h - 2)
             on_head(exponential, h - 1, 2)
 
             on_head(score_matmul, h, 1)
             on_head(transpose_query_and_key, h + 1)
             on_head(row_max, h, 0)
-            on_head(group_w, h)
+            on_head(group_w, h - 1)
             on_head(exponential, h - 1, 3)
             on_head(group_e, h - 1, 0)
 
             on_head(score_matmul, h, 2)
             on_head(transpose_e, h - 1, 1)
             on_head(row_max, h, 1)
-            on_head(quantise_value, h - 1)
+            on_head(quantise_value, h - 2)
             on_head(quantise_e, h - 2)
-            on_head(quantise_w, h)
+            on_head(quantise_w, h - 1)
             on_head(exponential, h, 0)
             on_head(copy_query_and_key, h + 1)
 
             on_head(score_matmul, h, 3)
             on_head(context, h - 2)
-            on_head(project_value, h)
+            on_head(project_value, h - 1)
             on_head(row_max, h, 2)
             on_head(exponential, h, 1)
             on_head(group_e, h - 1, 1)

@@ -44,7 +44,7 @@ def tile_fastbloomattention_pa_kernel(
     q_rows = query.rearrange("b h i d -> (b h) i d").rearrange("h (p ib) d -> p h (ib d)", ib=BLOCKS)
     k_rows = key.rearrange("b h j d -> (b h j) d").rearrange("(x p) d -> p x d", p=P)
     alibi_rows = alibi.rearrange("b h o j -> (b h o j)").rearrange("(x p) -> x p", p=P)
-    hs_rows = hidden_states.rearrange("b i k -> (b i) k").rearrange("(t p) k -> p t k", p=P)
+    hs_rows = hidden_states.rearrange("b i k -> (b i) k").rearrange("(u p x) k -> p u x k", p=P, x=2)
     w_rows = W_value.rearrange("(gu p e) n -> p gu e n", p=P, e=2)
     out_rows = out.rearrange("b i n -> (b i) n").rearrange("(p ib) n -> p ib n", ib=BLOCKS)
 
@@ -93,7 +93,7 @@ def tile_fastbloomattention_pa_kernel(
 
         hs_sb = const.tile([P, BLOCKS, HIDDEN], BF16)
         for t in range(BLOCKS):
-            nc.sync.dma_start(out=hs_sb[:, t, :], in_=hs_rows[:, t, :])
+            nc.sync.dma_start(out=hs_sb[:, t, :], in_=hs_rows[:, t // 2, t % 2, :])
         load_query_and_key(0, 1)
         load_query_and_key(1, GROUP)
         load_w(0)
@@ -239,22 +239,22 @@ def tile_fastbloomattention_pa_kernel(
             )
 
         def transpose_e(h, half):
-            e_ps = transpose_bank([P, 2, BLOCKS, P])
+            e_ps = psum.tile([P, 2, 2, P], F32, name="transpose_bank", tag="transpose_bank", bufs=2)
+            e_words = e_of[h][:].rearrange("p ib j -> p (ib j)").bitcast(F32)
             for x in range(2):
-                for t in range(BLOCKS):
-                    nc.tensor.transpose(
-                        e_ps[:, x, t, :], e_of[h][:, 2 * half + x, t * P : (t + 1) * P], ident_bf[:]
-                    )
+                for u in range(2):
+                    first = ((2 * half + x) * 2 + u) * P
+                    nc.tensor.transpose(e_ps[:, x, u, :], e_words[:, first : first + P], ident_f32[:])
             e_ps_of[(h, half)] = e_ps
 
         def group_e(h, half):
             if half == 0:
                 e_grouped_of[h] = work.tile(
-                    [P, BLOCKS, P, PACK], BF16, name="e_grouped", tag="e_grouped", align_bytes=64
+                    [P, BLOCKS, P, 2], F32, name="e_grouped", tag="e_grouped", align_bytes=64
                 )
             nc.scalar.copy(
                 out=e_grouped_of[h][:, 2 * half : 2 * half + 2, :, :],
-                in_=e_ps_of[(h, half)][:].rearrange("p x t m -> p x m t"),
+                in_=e_ps_of[(h, half)][:].rearrange("p x u m -> p x m u"),
             )
 
         def quantise_e(h):
@@ -263,7 +263,7 @@ def tile_fastbloomattention_pa_kernel(
             nc.vector.quantize_mx(
                 out=e_codes[:].bitcast(FP8X4),
                 scales=e_scales[:],
-                in_=e_grouped_of[h][:].rearrange("p ib m t -> p (ib m t)"),
+                in_=e_grouped_of[h][:].rearrange("p ib m u -> p (ib m u)").bitcast(BF16),
             )
             e_mx_of[h] = (e_codes, e_scales)
 

@@ -29,7 +29,7 @@ GROUP_COLS = GROUP * HEAD_DIM
 SCALE = 1.0 / math.sqrt(HEAD_DIM)
 INV_SCALE = math.sqrt(HEAD_DIM)
 
-DRAIN_STEPS = 3
+LAST_OFFSET = 13
 W_BUFFERS = 3
 
 FLOPS = 2 * SEQ * HIDDEN * HIDDEN + 2 * (2 * HEADS * SEQ * SEQ * HEAD_DIM)
@@ -52,7 +52,7 @@ def tile_fastbloomattention_pa_kernel(
         const = stack.enter_context(tc.tile_pool(name="const", bufs=1))
         weights = stack.enter_context(tc.tile_pool(name="weights", bufs=W_BUFFERS))
         work = stack.enter_context(tc.tile_pool(name="work", bufs=2))
-        stats = stack.enter_context(tc.tile_pool(name="stats", bufs=DRAIN_STEPS + 1))
+        stats = stack.enter_context(tc.tile_pool(name="stats", bufs=LAST_OFFSET // BLOCKS + 1))
         psum = stack.enter_context(tc.psum_pool(name="psum", bufs=1))
         stack.enter_context(tc.manual_schedule())
 
@@ -91,18 +91,23 @@ def tile_fastbloomattention_pa_kernel(
                     )
             w_raw_of[group] = w_raw
 
+        load_query_and_key(0, 1)
+        load_query_and_key(1, 2)
         hs_sb = const.tile([P, BLOCKS, HIDDEN], BF16)
         for t in range(BLOCKS):
             nc.sync.dma_start(out=hs_sb[:, t, :], in_=hs_rows[:, t // 2, t % 2, :])
-        load_query_and_key(0, 1)
-        load_query_and_key(1, GROUP)
         load_w(0)
+        load_query_and_key(2, GROUP)
         bias_sb = const.tile([P, HIDDEN], BF16)
         nc.sync.dma_start(out=bias_sb[:], in_=b_value.partition_broadcast(P))
         for group in range(1, GROUPS):
             load_query_and_key(group * GROUP, (group + 1) * GROUP)
             if group < W_BUFFERS:
                 load_w(group)
+
+        warm = const.tile([P, 1], F32)
+        nc.vector.memset(warm[:], 0.0)
+        nc.scalar.activation(out=warm[:], in_=warm[:], func=ACT.Exp)
 
         ident_bf = const.tile([P, P], BF16)
         make_identity(nc, ident_bf[:])
@@ -118,11 +123,12 @@ def tile_fastbloomattention_pa_kernel(
                     nc.tensor.transpose(
                         mask_ps[:, x, ib, :], mask_sb[:, ib, kb * P : (kb + 1) * P], ident_bf[:]
                     )
-            nc.scalar.copy(
+            copy_mask = nc.scalar.copy if half == 0 else nc.vector.tensor_copy
+            copy_mask(
                 out=mask_t[:, 2 * half : 2 * half + 2, :],
                 in_=mask_ps[:].rearrange("p x ib m -> p x (ib m)"),
             )
-        alibi_ps = transpose_bank([P, P])
+        alibi_ps = psum.tile([P, P], BF16, name="score_bank", tag="score_bank", bufs=4)
         nc.tensor.transpose(alibi_ps[:], alibi_sb[:], ident_bf[:])
         alibi_col = const.tile([P, HEADS * BLOCKS], F32)
         nc.vector.tensor_copy(out=alibi_col[:], in_=alibi_ps[:, 0 : HEADS * BLOCKS])
@@ -136,7 +142,8 @@ def tile_fastbloomattention_pa_kernel(
         def transpose_hidden_states(t):
             hs_words = hs_sb[:, t, :].bitcast(F32)
             for half in range(PASSES // 2):
-                hs_ps = score_bank([P, 2, 2, P])
+                bank = "v_ps" if half == 0 else "ctx_ps"
+                hs_ps = psum.tile([P, 2, 2, P], F32, name=bank, tag=bank)
                 for x in range(2):
                     for u in range(2):
                         first = (2 * half + x) * (K_PASS // 2) + u * P
@@ -161,11 +168,11 @@ def tile_fastbloomattention_pa_kernel(
         w_grouped_of, w_mx_of, v_ps_of, v_grouped_of, v_mx_of = {}, {}, {}, {}, {}
         ctx_ps_of = {}
 
-        def added_terms(h):
+        def added_terms(h, engine=nc.gpsimd):
             x_sb = work.tile([P, BLOCKS, SEQ], F32, name="x_sb", tag="x_sb")
             for kb in range(BLOCKS):
                 col = h * BLOCKS + kb
-                nc.gpsimd.tensor_scalar(
+                engine.tensor_scalar(
                     out=x_sb[:, kb, :],
                     in0=mask_t[:, kb, :],
                     scalar1=alibi_col[:, col : col + 1],
@@ -287,10 +294,12 @@ def tile_fastbloomattention_pa_kernel(
             )
             w_mx_of[h] = (w_codes, w_scales)
 
-        def project_value(h):
+        def project_value(h, half):
             w_codes, w_scales = w_mx_of[h]
-            v_ps = psum.tile([P, BLOCKS, HEAD_DIM], F32, name="v_ps", tag="v_ps")
-            for t in range(BLOCKS):
+            if half == 0:
+                v_ps_of[h] = psum.tile([P, BLOCKS, HEAD_DIM], F32, name="v_ps", tag="v_ps")
+            v_ps = v_ps_of[h]
+            for t in range(2 * half, 2 * half + 2):
                 for g in range(PASSES):
                     nc.tensor.matmul_mx(
                         out=v_ps[:, t, :],
@@ -301,7 +310,6 @@ def tile_fastbloomattention_pa_kernel(
                         start=(g == 0),
                         stop=(g == PASSES - 1),
                     )
-            v_ps_of[h] = v_ps
 
         def group_value(h):
             v_grouped = work.tile([P, HEAD_DIM, PACK], BF16, name="v_grouped", tag="v_grouped", align_bytes=64)
@@ -338,63 +346,63 @@ def tile_fastbloomattention_pa_kernel(
                 )
             ctx_ps_of[h] = ctx_ps
 
-        def divide(h):
+        inv_sum_of = {}
+
+        def invert_sums(h):
             inv_sum = stats.tile([P, BLOCKS], F32, name="inv_sum", tag="inv_sum")
             nc.vector.reciprocal(out=inv_sum[:], in_=row_sum_of[h][:])
+            inv_sum_of[h] = inv_sum
+
+        def divide(h):
             out_sb = work.tile([P, BLOCKS, HEAD_DIM], F32, name="out_sb", tag="out_sb")
-            nc.vector.tensor_tensor(
-                out=out_sb[:],
-                in0=ctx_ps_of[h][:],
-                in1=inv_sum[:].unsqueeze(2).to_broadcast([P, BLOCKS, HEAD_DIM]),
-                op=ALU.mult,
-            )
+            for ib in range(BLOCKS):
+                nc.scalar.activation(
+                    out=out_sb[:, ib, :],
+                    in_=ctx_ps_of[h][:, ib, :],
+                    func=ACT.Copy,
+                    scale=inv_sum_of[h][:, ib : ib + 1],
+                )
             nc.sync.dma_start(out=out_rows[:, :, h * HEAD_DIM : (h + 1) * HEAD_DIM], in_=out_sb[:])
 
-        def on_block(piece, t):
-            if 0 <= t < BLOCKS:
-                piece(t)
-
-        def on_head(piece, h, *args):
-            if 0 <= h < HEADS:
+        def run(slot, offset, piece, *args):
+            h, rest = divmod(slot - offset, BLOCKS)
+            if rest == 0 and 0 <= h < HEADS:
                 piece(h, *args)
 
-        added_terms(0)
-        for t in range(BLOCKS + 2):
-            on_block(transpose_hidden_states, t)
-            on_block(group_hidden_states, t - 1)
-            on_block(quantise_hidden_states, t - 2)
+        def run_block(slot, offset, piece):
+            if 0 <= slot - offset < BLOCKS:
+                piece(slot - offset)
+
         transpose_query_and_key(0)
         copy_query_and_key(0)
+        added_terms(0, engine=nc.vector)
 
-        for h in range(HEADS + DRAIN_STEPS):
-            on_head(added_terms, h + 1)
+        for slot in range(BLOCKS * HEADS + LAST_OFFSET + 1):
+            run(slot, -4, added_terms)
 
-            on_head(score_matmul, h, 0)
-            on_head(transpose_e, h - 1, 0)
-            on_head(row_max, h - 1, 3)
-            on_head(divide, h - 3)
-            on_head(group_value, h - 2)
-            on_head(exponential, h - 1, 2)
+            for ib in range(BLOCKS):
+                run(slot, ib, score_matmul, ib)
+            run(slot, 5, project_value, 0)
+            run(slot, 7, project_value, 1)
+            run(slot, 12, context)
+            run(slot, 4, transpose_e, 0)
+            run(slot, -3, transpose_query_and_key)
+            run(slot, 6, transpose_e, 1)
+            run_block(slot, 0, transpose_hidden_states)
 
-            on_head(score_matmul, h, 1)
-            on_head(transpose_query_and_key, h + 1)
-            on_head(row_max, h, 0)
-            on_head(group_w, h - 1)
-            on_head(exponential, h - 1, 3)
-            on_head(group_e, h - 1, 0)
+            for ib in range(BLOCKS):
+                run(slot, ib + 1, row_max, ib)
+                run(slot, ib + 2, exponential, ib)
+            run_block(slot, 1, group_hidden_states)
+            run(slot, 8, group_value)
+            run(slot, 8, invert_sums)
+            run(slot, 10, quantise_value)
+            run(slot, 2, group_w)
+            run(slot, 11, quantise_e)
+            run(slot, 3, quantise_w)
+            run_block(slot, 2, quantise_hidden_states)
 
-            on_head(score_matmul, h, 2)
-            on_head(transpose_e, h - 1, 1)
-            on_head(row_max, h, 1)
-            on_head(quantise_value, h - 2)
-            on_head(quantise_e, h - 2)
-            on_head(quantise_w, h - 1)
-            on_head(exponential, h, 0)
-            on_head(copy_query_and_key, h + 1)
-
-            on_head(score_matmul, h, 3)
-            on_head(context, h - 2)
-            on_head(project_value, h - 1)
-            on_head(row_max, h, 2)
-            on_head(exponential, h, 1)
-            on_head(group_e, h - 1, 1)
+            run(slot, 5, group_e, 0)
+            run(slot, -2, copy_query_and_key)
+            run(slot, 7, group_e, 1)
+            run(slot, 13, divide)

@@ -30,6 +30,7 @@ SCALE = 1.0 / math.sqrt(HEAD_DIM)
 INV_SCALE = math.sqrt(HEAD_DIM)
 
 LAST_OFFSET = 13
+PROJECT_PARTS = ((0, 5), (5, 11), (11, 16))
 W_BUFFERS = 3
 
 FLOPS = 2 * SEQ * HIDDEN * HIDDEN + 2 * (2 * HEADS * SEQ * SEQ * HEAD_DIM)
@@ -294,22 +295,22 @@ def tile_fastbloomattention_pa_kernel(
             )
             w_mx_of[h] = (w_codes, w_scales)
 
-        def project_value(h, half):
+        def project_value(h, part):
             w_codes, w_scales = w_mx_of[h]
-            if half == 0:
+            if part == 0:
                 v_ps_of[h] = psum.tile([P, BLOCKS, HEAD_DIM], F32, name="v_ps", tag="v_ps")
             v_ps = v_ps_of[h]
-            for t in range(2 * half, 2 * half + 2):
-                for g in range(PASSES):
-                    nc.tensor.matmul_mx(
-                        out=v_ps[:, t, :],
-                        lhsT=hs_codes[:, t, g, :].bitcast(FP8X4),
-                        lhsT_scale=hs_scales[:, t, g, :],
-                        rhs=w_codes[:, g, :].bitcast(FP8X4),
-                        rhs_scale=w_scales[:, g, :],
-                        start=(g == 0),
-                        stop=(g == PASSES - 1),
-                    )
+            for n in range(*PROJECT_PARTS[part]):
+                t, g = divmod(n, PASSES)
+                nc.tensor.matmul_mx(
+                    out=v_ps[:, t, :],
+                    lhsT=hs_codes[:, t, g, :].bitcast(FP8X4),
+                    lhsT_scale=hs_scales[:, t, g, :],
+                    rhs=w_codes[:, g, :].bitcast(FP8X4),
+                    rhs_scale=w_scales[:, g, :],
+                    start=(g == 0),
+                    stop=(g == PASSES - 1),
+                )
 
         def group_value(h):
             v_grouped = work.tile([P, HEAD_DIM, PACK], BF16, name="v_grouped", tag="v_grouped", align_bytes=64)
@@ -382,8 +383,8 @@ def tile_fastbloomattention_pa_kernel(
 
             for ib in range(BLOCKS):
                 run(slot, ib, score_matmul, ib)
-            run(slot, 5, project_value, 0)
-            run(slot, 7, project_value, 1)
+            for part in range(len(PROJECT_PARTS)):
+                run(slot, 5 + part, project_value, part)
             run(slot, 12, context)
             run(slot, 4, transpose_e, 0)
             run(slot, -3, transpose_query_and_key)

@@ -22,9 +22,9 @@ HEAD_DIM = 128
 HIDDEN = HEADS * HEAD_DIM
 BLOCKS = SEQ // P
 PASSES = HIDDEN // K_PASS
-GROUP = 4
-GROUPS = HEADS // GROUP
-GROUP_COLS = GROUP * HEAD_DIM
+GROUP_STARTS = (0, 1, 4, 8, 12)
+GROUP_STOPS = GROUP_STARTS[1:] + (HEADS,)
+GROUPS = len(GROUP_STARTS)
 
 SCALE = 1.0 / math.sqrt(HEAD_DIM)
 INV_SCALE = math.sqrt(HEAD_DIM)
@@ -63,8 +63,8 @@ def tile_fastbloomattention_pa_kernel(
         def transpose_bank(shape):
             return psum.tile(shape, BF16, name="transpose_bank", tag="transpose_bank", bufs=2)
 
-        def head_cols(h):
-            return slice((h % GROUP) * HEAD_DIM, (h % GROUP + 1) * HEAD_DIM)
+        def head_cols(h, first=0):
+            return slice((h - first) * HEAD_DIM, (h - first + 1) * HEAD_DIM)
 
         mask_sb = const.tile([P, BLOCKS, SEQ], BF16)
         nc.sync.dma_start(out=mask_sb[:], in_=mask_rows)
@@ -83,8 +83,8 @@ def tile_fastbloomattention_pa_kernel(
         w_raw_of = {}
 
         def load_w(group):
-            w_raw = weights.tile([P, PASSES, PACK, GROUP_COLS], BF16, name="w_raw", tag="w_raw")
-            cols = slice(group * GROUP_COLS, (group + 1) * GROUP_COLS)
+            cols = slice(GROUP_STARTS[group] * HEAD_DIM, GROUP_STOPS[group] * HEAD_DIM)
+            w_raw = weights.tile([P, PASSES, PACK, cols.stop - cols.start], BF16, name="w_raw", tag="w_raw")
             for g in range(PASSES):
                 for u in range(2):
                     nc.sync.dma_start(
@@ -98,13 +98,24 @@ def tile_fastbloomattention_pa_kernel(
         for t in range(BLOCKS):
             nc.sync.dma_start(out=hs_sb[:, t, :], in_=hs_rows[:, t // 2, t % 2, :])
         load_w(0)
-        load_query_and_key(2, GROUP)
+        load_query_and_key(2, 4)
+        load_w(1)
         bias_sb = const.tile([P, HIDDEN], BF16)
         nc.sync.dma_start(out=bias_sb[:], in_=b_value.partition_broadcast(P))
-        for group in range(1, GROUPS):
-            load_query_and_key(group * GROUP, (group + 1) * GROUP)
+        for group in range(2, GROUPS):
+            load_query_and_key(GROUP_STARTS[group], GROUP_STOPS[group])
             if group < W_BUFFERS:
                 load_w(group)
+
+        zeros = const.tile([P, SEQ], BF16)
+        nc.vector.memset(zeros[:], 0.0)
+
+        def keep_clock(count):
+            idle_ps = psum.tile([P, SEQ], F32, name="transpose_bank", tag="transpose_bank", bufs=2)
+            for turn in range(count):
+                nc.tensor.matmul(out=idle_ps[:], lhsT=zeros[:, 0:P], rhs=zeros[:], start=True, stop=True)
+
+        keep_clock(6)
 
         warm = const.tile([P, 1], F32)
         nc.vector.memset(warm[:], 0.0)
@@ -276,14 +287,15 @@ def tile_fastbloomattention_pa_kernel(
             e_mx_of[h] = (e_codes, e_scales)
 
         def group_w(h):
+            group = max(g for g in range(GROUPS) if GROUP_STARTS[g] <= h)
             w_grouped = work.tile([P, PASSES, HEAD_DIM, PACK], BF16, name="w_grouped", tag="w_grouped", align_bytes=64)
             nc.vector.tensor_copy(
                 out=w_grouped[:].rearrange("p g (c i) t -> p g c t i", i=4),
-                in_=w_raw_of[h // GROUP][:, :, :, head_cols(h)].rearrange("p g t (c i) -> p g c t i", i=4),
+                in_=w_raw_of[group][:, :, :, head_cols(h, GROUP_STARTS[group])].rearrange("p g t (c i) -> p g c t i", i=4),
             )
             w_grouped_of[h] = w_grouped
-            if h % GROUP == GROUP - 1 and h // GROUP + W_BUFFERS < GROUPS:
-                load_w(h // GROUP + W_BUFFERS)
+            if h == GROUP_STOPS[group] - 1 and group + W_BUFFERS < GROUPS:
+                load_w(group + W_BUFFERS)
 
         def quantise_w(h):
             w_codes = work.tile([P, PASSES, HEAD_DIM], U32, name="w_codes", tag="w_codes", align_bytes=64)
@@ -314,7 +326,7 @@ def tile_fastbloomattention_pa_kernel(
 
         def group_value(h):
             v_grouped = work.tile([P, HEAD_DIM, PACK], BF16, name="v_grouped", tag="v_grouped", align_bytes=64)
-            bias = bias_sb[:, h * HEAD_DIM : (h + 1) * HEAD_DIM].unsqueeze(2).to_broadcast([P, HEAD_DIM, PACK])
+            bias = bias_sb[:, head_cols(h)].unsqueeze(2).to_broadcast([P, HEAD_DIM, PACK])
             nc.vector.tensor_tensor(
                 out=v_grouped[:], in0=v_ps_of[h][:].rearrange("p t d -> p d t"), in1=bias, op=ALU.add
             )
@@ -363,7 +375,7 @@ def tile_fastbloomattention_pa_kernel(
                     func=ACT.Copy,
                     scale=inv_sum_of[h][:, ib : ib + 1],
                 )
-            nc.sync.dma_start(out=out_rows[:, :, h * HEAD_DIM : (h + 1) * HEAD_DIM], in_=out_sb[:])
+            nc.sync.dma_start(out=out_rows[:, :, head_cols(h)], in_=out_sb[:])
 
         def run(slot, offset, piece, *args):
             h, rest = divmod(slot - offset, BLOCKS)
@@ -375,6 +387,7 @@ def tile_fastbloomattention_pa_kernel(
                 piece(slot - offset)
 
         transpose_query_and_key(0)
+        keep_clock(3)
         copy_query_and_key(0)
         added_terms(0, engine=nc.vector)
 
@@ -386,6 +399,8 @@ def tile_fastbloomattention_pa_kernel(
             for part in range(len(PROJECT_PARTS)):
                 run(slot, 5 + part, project_value, part)
             run(slot, 12, context)
+            if slot < 5:
+                keep_clock(1)
             run(slot, 4, transpose_e, 0)
             run(slot, -3, transpose_query_and_key)
             run(slot, 6, transpose_e, 1)
@@ -398,9 +413,15 @@ def tile_fastbloomattention_pa_kernel(
             run(slot, 8, group_value)
             run(slot, 8, invert_sums)
             run(slot, 10, quantise_value)
-            run(slot, 2, group_w)
+            if slot == 3:
+                group_w(0)
+            elif slot != 2:
+                run(slot, 2, group_w)
             run(slot, 11, quantise_e)
-            run(slot, 3, quantise_w)
+            if slot == 4:
+                quantise_w(0)
+            elif slot != 3:
+                run(slot, 3, quantise_w)
             run_block(slot, 2, quantise_hidden_states)
 
             run(slot, 5, group_e, 0)

@@ -57,6 +57,9 @@ def tile_fastbloomattention_pa_kernel(
         psum = stack.enter_context(tc.psum_pool(name="psum", bufs=1))
         stack.enter_context(tc.manual_schedule())
 
+        def context_bank(shape):
+            return psum.tile(shape, F32, name="ctx_ps", tag="ctx_ps")
+
         def score_bank(shape):
             return psum.tile(shape, F32, name="score_bank", tag="score_bank", bufs=4)
 
@@ -66,11 +69,13 @@ def tile_fastbloomattention_pa_kernel(
         def head_cols(h, first=0):
             return slice((h - first) * HEAD_DIM, (h - first + 1) * HEAD_DIM)
 
-        mask_sb = const.tile([P, BLOCKS, SEQ], BF16)
-        nc.sync.dma_start(out=mask_sb[:], in_=mask_rows)
         alibi_sb = const.tile([P, P], BF16)
         nc.vector.memset(alibi_sb[:], 0.0)
         nc.sync.dma_start(out=alibi_sb[0 : HEADS * BLOCKS, :], in_=alibi_rows)
+        mask_sb = const.tile([P, BLOCKS, SEQ], BF16)
+        for half in range(2):
+            keys = slice(half * SEQ // 2, (half + 1) * SEQ // 2)
+            nc.sync.dma_start(out=mask_sb[:, :, keys], in_=mask_rows[:, :, keys])
 
         q_sb = const.tile([P, HEADS, BLOCKS * HEAD_DIM], BF16)
         k_sb = const.tile([P, HEADS * BLOCKS, HEAD_DIM], BF16)
@@ -126,6 +131,10 @@ def tile_fastbloomattention_pa_kernel(
         ident_f32 = const.tile([P, P], F32)
         make_identity(nc, ident_f32[:])
 
+        alibi_ps = psum.tile([P, P], BF16, name="score_bank", tag="score_bank", bufs=4)
+        nc.tensor.transpose(alibi_ps[:], alibi_sb[:], ident_bf[:])
+        alibi_col = const.tile([P, HEADS * BLOCKS], F32)
+        nc.vector.tensor_copy(out=alibi_col[:], in_=alibi_ps[:, 0 : HEADS * BLOCKS])
         mask_t = const.tile([P, BLOCKS, SEQ], BF16)
         for half in range(2):
             mask_ps = transpose_bank([P, 2, BLOCKS, P])
@@ -135,15 +144,10 @@ def tile_fastbloomattention_pa_kernel(
                     nc.tensor.transpose(
                         mask_ps[:, x, ib, :], mask_sb[:, ib, kb * P : (kb + 1) * P], ident_bf[:]
                     )
-            copy_mask = nc.scalar.copy if half == 0 else nc.vector.tensor_copy
-            copy_mask(
+            nc.scalar.copy(
                 out=mask_t[:, 2 * half : 2 * half + 2, :],
                 in_=mask_ps[:].rearrange("p x ib m -> p x (ib m)"),
             )
-        alibi_ps = psum.tile([P, P], BF16, name="score_bank", tag="score_bank", bufs=4)
-        nc.tensor.transpose(alibi_ps[:], alibi_sb[:], ident_bf[:])
-        alibi_col = const.tile([P, HEADS * BLOCKS], F32)
-        nc.vector.tensor_copy(out=alibi_col[:], in_=alibi_ps[:, 0 : HEADS * BLOCKS])
 
         hs_grouped = const.tile([P, BLOCKS, PASSES, P, 2], F32, align_bytes=64)
         hs_codes = const.tile([P, BLOCKS, PASSES, P], U32, align_bytes=64)
@@ -276,15 +280,18 @@ def tile_fastbloomattention_pa_kernel(
                 in_=e_ps_of[(h, half)][:].rearrange("p x u m -> p x m u"),
             )
 
-        def quantise_e(h):
-            e_codes = work.tile([P, SEQ], U32, name="e_codes", tag="e_codes", align_bytes=64)
-            e_scales = work.tile([P, SEQ], U8, name="e_scales", tag="e_scales", align_bytes=64)
+        def quantise_e(h, first=0, stop=BLOCKS):
+            if first == 0:
+                e_codes = work.tile([P, SEQ], U32, name="e_codes", tag="e_codes", align_bytes=64)
+                e_scales = work.tile([P, SEQ], U8, name="e_scales", tag="e_scales", align_bytes=64)
+                e_mx_of[h] = (e_codes, e_scales)
+            e_codes, e_scales = e_mx_of[h]
+            queries = slice(first * P, stop * P)
             nc.vector.quantize_mx(
-                out=e_codes[:].bitcast(FP8X4),
-                scales=e_scales[:],
-                in_=e_grouped_of[h][:].rearrange("p ib m u -> p (ib m u)").bitcast(BF16),
+                out=e_codes[:, queries].bitcast(FP8X4),
+                scales=e_scales[:, queries],
+                in_=e_grouped_of[h][:, first:stop].rearrange("p ib m u -> p (ib m u)").bitcast(BF16),
             )
-            e_mx_of[h] = (e_codes, e_scales)
 
         def group_w(h):
             group = max(g for g in range(GROUPS) if GROUP_STARTS[g] <= h)
@@ -342,14 +349,14 @@ def tile_fastbloomattention_pa_kernel(
             )
             v_mx_of[h] = (v_codes, v_scales)
 
-        def context(h):
+        def context(h, bank, first=0, stop=BLOCKS):
             e_codes, e_scales = e_mx_of[h]
             v_codes, v_scales = v_mx_of[h]
-            ctx_ps = psum.tile([P, BLOCKS, HEAD_DIM], F32, name="ctx_ps", tag="ctx_ps")
-            for ib in range(BLOCKS):
+            ctx_ps = bank([P, stop - first, HEAD_DIM])
+            for ib in range(first, stop):
                 queries = slice(ib * P, (ib + 1) * P)
                 nc.tensor.matmul_mx(
-                    out=ctx_ps[:, ib, :],
+                    out=ctx_ps[:, ib - first, :],
                     lhsT=e_codes[:, queries].bitcast(FP8X4),
                     lhsT_scale=e_scales[:, queries],
                     rhs=v_codes[:].bitcast(FP8X4),
@@ -357,7 +364,7 @@ def tile_fastbloomattention_pa_kernel(
                     start=True,
                     stop=True,
                 )
-            ctx_ps_of[h] = ctx_ps
+            ctx_ps_of[(h, first)] = ctx_ps
 
         inv_sum_of = {}
 
@@ -366,30 +373,47 @@ def tile_fastbloomattention_pa_kernel(
             nc.vector.reciprocal(out=inv_sum[:], in_=row_sum_of[h][:])
             inv_sum_of[h] = inv_sum
 
-        def divide(h):
+        def divide(h, stop=BLOCKS):
             out_sb = work.tile([P, BLOCKS, HEAD_DIM], F32, name="out_sb", tag="out_sb")
-            for ib in range(BLOCKS):
+            for ib in range(stop):
                 nc.scalar.activation(
                     out=out_sb[:, ib, :],
-                    in_=ctx_ps_of[h][:, ib, :],
+                    in_=ctx_ps_of[(h, 0)][:, ib, :],
                     func=ACT.Copy,
                     scale=inv_sum_of[h][:, ib : ib + 1],
                 )
-            nc.sync.dma_start(out=out_rows[:, :, head_cols(h)], in_=out_sb[:])
+            nc.sync.dma_start(out=out_rows[:, 0:stop, head_cols(h)], in_=out_sb[:, 0:stop, :])
 
-        def run(slot, offset, piece, *args):
+        def divide_rest(h, first):
+            rest = BLOCKS - first
+            rest_sb = work.tile([P, rest, HEAD_DIM], F32, name="rest_sb", tag="rest_sb", bufs=1)
+            nc.vector.tensor_tensor(
+                out=rest_sb[:],
+                in0=ctx_ps_of[(h, first)][:],
+                in1=inv_sum_of[h][:, first:].unsqueeze(2).to_broadcast([P, rest, HEAD_DIM]),
+                op=ALU.mult,
+            )
+            nc.sync.dma_start(out=out_rows[:, first:, head_cols(h)], in_=rest_sb[:])
+
+        last = HEADS - 1
+
+        def run(slot, offset, piece, *args, heads=range(HEADS)):
             h, rest = divmod(slot - offset, BLOCKS)
-            if rest == 0 and 0 <= h < HEADS:
+            if rest == 0 and h in heads:
                 piece(h, *args)
+
+        def run_last(slot, offset, piece, *args):
+            if slot - offset == BLOCKS * last:
+                piece(last, *args)
 
         def run_block(slot, offset, piece):
             if 0 <= slot - offset < BLOCKS:
                 piece(slot - offset)
 
+        added_terms(0, engine=nc.vector)
         transpose_query_and_key(0)
         keep_clock(3)
         copy_query_and_key(0)
-        added_terms(0, engine=nc.vector)
 
         for slot in range(BLOCKS * HEADS + LAST_OFFSET + 1):
             run(slot, -4, added_terms)
@@ -398,12 +422,14 @@ def tile_fastbloomattention_pa_kernel(
                 run(slot, ib, score_matmul, ib)
             for part in range(len(PROJECT_PARTS)):
                 run(slot, 5 + part, project_value, part)
-            run(slot, 12, context)
+            run(slot, 12, context, context_bank, heads=range(last))
+            run_last(slot, 11, context, score_bank, 0, 2)
+            run_last(slot, 12, context, score_bank, 2, BLOCKS)
             if slot < 5:
                 keep_clock(1)
-            run(slot, 4, transpose_e, 0)
-            run(slot, -3, transpose_query_and_key)
-            run(slot, 6, transpose_e, 1)
+            run(slot, -4, transpose_query_and_key)
+            run(slot, 5, transpose_e, 0)
+            run(slot, 7, transpose_e, 1)
             run_block(slot, 0, transpose_hidden_states)
 
             for ib in range(BLOCKS):
@@ -417,14 +443,18 @@ def tile_fastbloomattention_pa_kernel(
                 group_w(0)
             elif slot != 2:
                 run(slot, 2, group_w)
-            run(slot, 11, quantise_e)
+            run(slot, 10, quantise_e, heads=range(last))
+            run_last(slot, 8, quantise_e, 0, 2)
+            run_last(slot, 10, quantise_e, 2, BLOCKS)
             if slot == 4:
                 quantise_w(0)
             elif slot != 3:
                 run(slot, 3, quantise_w)
             run_block(slot, 2, quantise_hidden_states)
 
-            run(slot, 5, group_e, 0)
-            run(slot, -2, copy_query_and_key)
-            run(slot, 7, group_e, 1)
-            run(slot, 13, divide)
+            run(slot, -3, copy_query_and_key)
+            run(slot, 6, group_e, 0)
+            run(slot, 8, group_e, 1)
+            run(slot, 13, divide, heads=range(last))
+            run_last(slot, 12, divide, 2)
+            run_last(slot, 13, divide_rest, 2)

import math
from contextlib import ExitStack

import concourse.mybir as mybir
from concourse.masks import make_identity

F32 = mybir.dt.float32
BF16 = mybir.dt.bfloat16
U8 = mybir.dt.uint8
U32 = mybir.dt.uint32
FP8X4 = mybir.dt.float8_e4m3fn_x4
ALU = mybir.AluOpType
ACT = mybir.ActivationFunctionType

P = 128
PACK = 4
K_PASS = P * PACK

SEQ = 512
HEADS = 16
HEAD_DIM = 128
HIDDEN = HEADS * HEAD_DIM
BLOCKS = SEQ // P
PASSES = HIDDEN // K_PASS
GROUP_STARTS = (0, 1, 4, 8, 12)
GROUP_STOPS = GROUP_STARTS[1:] + (HEADS,)
GROUPS = len(GROUP_STARTS)

SCALE = 1.0 / math.sqrt(HEAD_DIM)
INV_SCALE = math.sqrt(HEAD_DIM)

LAST_OFFSET = 13
PROJECT_PARTS = ((0, 5), (5, 11), (11, 16))
W_BUFFERS = 3

FLOPS = 2 * SEQ * HIDDEN * HIDDEN + 2 * (2 * HEADS * SEQ * SEQ * HEAD_DIM)


def tile_fastbloomattention_pa_kernel(
    tc, hidden_states, W_value, b_value, query, key, alibi, attention_mask, out
):
    nc = tc.nc

    mask_rows = attention_mask.rearrange("a b i j -> (a b i) j").rearrange("(p ib) j -> p ib j", ib=BLOCKS)
    q_rows = query.rearrange("b h i d -> (b h) i d").rearrange("h (p ib) d -> p h (ib d)", ib=BLOCKS)
    k_rows = key.rearrange("b h j d -> (b h j) d").rearrange("(x p) d -> p x d", p=P)
    alibi_rows = alibi.rearrange("b h o j -> (b h o j)").rearrange("(x p) -> x p", p=P)
    hs_rows = hidden_states.rearrange("b i k -> (b i) k").rearrange("(u p x) k -> p u x k", p=P, x=2)
    w_rows = W_value.rearrange("(gu p e) n -> p gu e n", p=P, e=2)
    out_rows = out.rearrange("b i n -> (b i) n").rearrange("(p ib) n -> p ib n", ib=BLOCKS)

    with ExitStack() as stack:
        const = stack.enter_context(tc.tile_pool(name="const", bufs=1))
        weights = stack.enter_context(tc.tile_pool(name="weights", bufs=W_BUFFERS))
        work = stack.enter_context(tc.tile_pool(name="work", bufs=2))
        stats = stack.enter_context(tc.tile_pool(name="stats", bufs=LAST_OFFSET // BLOCKS + 1))
        psum = stack.enter_context(tc.psum_pool(name="psum", bufs=1))
        stack.enter_context(tc.manual_schedule())

        def context_bank(shape):
            return psum.tile(shape, F32, name="ctx_ps", tag="ctx_ps")

        def score_bank(shape):
            return psum.tile(shape, F32, name="score_bank", tag="score_bank", bufs=4)

        def transpose_bank(shape):
            return psum.tile(shape, BF16, name="transpose_bank", tag="transpose_bank", bufs=2)

        def head_cols(h, first=0):
            return slice((h - first) * HEAD_DIM, (h - first + 1) * HEAD_DIM)

        alibi_sb = const.tile([P, P], BF16)
        nc.vector.memset(alibi_sb[:], 0.0)
        nc.sync.dma_start(out=alibi_sb[0 : HEADS * BLOCKS, :], in_=alibi_rows)
        mask_sb = const.tile([P, BLOCKS, SEQ], BF16)
        for half in range(2):
            keys = slice(half * SEQ // 2, (half + 1) * SEQ // 2)
            nc.sync.dma_start(out=mask_sb[:, :, keys], in_=mask_rows[:, :, keys])

        q_sb = const.tile([P, HEADS, BLOCKS * HEAD_DIM], BF16)
        k_sb = const.tile([P, HEADS * BLOCKS, HEAD_DIM], BF16)

        def load_query_and_key(first, stop):
            nc.sync.dma_start(out=q_sb[:, first:stop, :], in_=q_rows[:, first:stop, :])
            blocks = slice(first * BLOCKS, stop * BLOCKS)
            nc.sync.dma_start(out=k_sb[:, blocks, :], in_=k_rows[:, blocks, :])

        w_raw_of = {}

        def load_w(group):
            cols = slice(GROUP_STARTS[group] * HEAD_DIM, GROUP_STOPS[group] * HEAD_DIM)
            w_raw = weights.tile([P, PASSES, PACK, cols.stop - cols.start], BF16, name="w_raw", tag="w_raw")
            for g in range(PASSES):
                for u in range(2):
                    nc.sync.dma_start(
                        out=w_raw[:, g, 2 * u : 2 * u + 2, :], in_=w_rows[:, 2 * g + u, :, cols]
                    )
            w_raw_of[group] = w_raw

        load_query_and_key(0, 1)
        load_query_and_key(1, 2)
        hs_sb = const.tile([P, BLOCKS, HIDDEN], BF16)
        for t in range(BLOCKS):
            nc.sync.dma_start(out=hs_sb[:, t, :], in_=hs_rows[:, t // 2, t % 2, :])
        load_w(0)
        load_query_and_key(2, 4)
        load_w(1)
        bias_sb = const.tile([P, HIDDEN], BF16)
        nc.sync.dma_start(out=bias_sb[:], in_=b_value.partition_broadcast(P))
        for group in range(2, GROUPS):
            load_query_and_key(GROUP_STARTS[group], GROUP_STOPS[group])
            if group < W_BUFFERS:
                load_w(group)

        zeros = const.tile([P, SEQ], BF16)
        nc.vector.memset(zeros[:], 0.0)

        def keep_clock(count):
            idle_ps = psum.tile([P, SEQ], F32, name="transpose_bank", tag="transpose_bank", bufs=2)
            for turn in range(count):
                nc.tensor.matmul(out=idle_ps[:], lhsT=zeros[:, 0:P], rhs=zeros[:], start=True, stop=True)

        keep_clock(6)

        warm = const.tile([P, 1], F32)
        nc.vector.memset(warm[:], 0.0)
        nc.scalar.activation(out=warm[:], in_=warm[:], func=ACT.Exp)

        ident_bf = const.tile([P, P], BF16)
        make_identity(nc, ident_bf[:])
        ident_f32 = const.tile([P, P], F32)
        make_identity(nc, ident_f32[:])

        alibi_ps = psum.tile([P, P], BF16, name="score_bank", tag="score_bank", bufs=4)
        nc.tensor.transpose(alibi_ps[:], alibi_sb[:], ident_bf[:])
        alibi_col = const.tile([P, HEADS * BLOCKS], F32)
        nc.vector.tensor_copy(out=alibi_col[:], in_=alibi_ps[:, 0 : HEADS * BLOCKS])
        mask_t = const.tile([P, BLOCKS, SEQ], BF16)
        for half in range(2):
            mask_ps = transpose_bank([P, 2, BLOCKS, P])
            for x in range(2):
                kb = 2 * half + x
                for ib in range(BLOCKS):
                    nc.tensor.transpose(
                        mask_ps[:, x, ib, :], mask_sb[:, ib, kb * P : (kb + 1) * P], ident_bf[:]
                    )
            nc.scalar.copy(
                out=mask_t[:, 2 * half : 2 * half + 2, :],
                in_=mask_ps[:].rearrange("p x ib m -> p x (ib m)"),
            )

        hs_grouped = const.tile([P, BLOCKS, PASSES, P, 2], F32, align_bytes=64)
        hs_codes = const.tile([P, BLOCKS, PASSES, P], U32, align_bytes=64)
        hs_scales = const.tile([P, BLOCKS, PASSES, P], U8, align_bytes=64)

        hs_ps_of = {}

        def transpose_hidden_states(t):
            hs_words = hs_sb[:, t, :].bitcast(F32)
            for half in range(PASSES // 2):
                bank = "v_ps" if half == 0 else "ctx_ps"
                hs_ps = psum.tile([P, 2, 2, P], F32, name=bank, tag=bank)
                for x in range(2):
                    for u in range(2):
                        first = (2 * half + x) * (K_PASS // 2) + u * P
                        nc.tensor.transpose(hs_ps[:, x, u, :], hs_words[:, first : first + P], ident_f32[:])
                hs_ps_of[(t, half)] = hs_ps

        def group_hidden_states(t):
            nc.scalar.copy(out=hs_grouped[:, t, 0:2, :, :], in_=hs_ps_of[(t, 0)][:].rearrange("p x u m -> p x m u"))
            nc.vector.tensor_copy(
                out=hs_grouped[:, t, 2:4, :, :], in_=hs_ps_of[(t, 1)][:].rearrange("p x u m -> p x m u")
            )

        def quantise_hidden_states(t):
            nc.vector.quantize_mx(
                out=hs_codes[:, t].rearrange("p g m -> p (g m)").bitcast(FP8X4),
                scales=hs_scales[:, t].rearrange("p g m -> p (g m)"),
                in_=hs_grouped[:, t].rearrange("p g m u -> p (g m u)").bitcast(BF16),
            )

        x_of, qk_ps_of, qk_t_of, s_ps_of, e_of, shift_of, row_sum_of = {}, {}, {}, {}, {}, {}, {}
        e_ps_of, e_grouped_of, e_mx_of = {}, {}, {}
        w_grouped_of, w_mx_of, v_ps_of, v_grouped_of, v_mx_of = {}, {}, {}, {}, {}
        ctx_ps_of = {}

        def added_terms(h, engine=nc.gpsimd):
            x_sb = work.tile([P, BLOCKS, SEQ], F32, name="x_sb", tag="x_sb")
            for kb in range(BLOCKS):
                col = h * BLOCKS + kb
                engine.tensor_scalar(
                    out=x_sb[:, kb, :],
                    in0=mask_t[:, kb, :],
                    scalar1=alibi_col[:, col : col + 1],
                    scalar2=INV_SCALE,
                    op0=ALU.add,
                    op1=ALU.mult,
                )
            x_of[h] = x_sb

        def transpose_query_and_key(h):
            qk_ps = transpose_bank([P, 2 * BLOCKS, P])
            for ib in range(BLOCKS):
                nc.tensor.transpose(
                    qk_ps[:, ib, :], q_sb[:, h, ib * HEAD_DIM : (ib + 1) * HEAD_DIM], ident_bf[:]
                )
            for kb in range(BLOCKS):
                nc.tensor.transpose(qk_ps[:, BLOCKS + kb, :], k_sb[:, h * BLOCKS + kb, :], ident_bf[:])
            qk_ps_of[h] = qk_ps

        def copy_query_and_key(h):
            qk_t = work.tile([P, 2 * BLOCKS, P], BF16, name="qk_t", tag="qk_t")
            nc.scalar.copy(out=qk_t[:], in_=qk_ps_of[h][:])
            qk_t_of[h] = qk_t

        def score_matmul(h, ib):
            if ib == 0:
                e_of[h] = work.tile([P, BLOCKS, SEQ], BF16, name="e_sb", tag="e_sb")
                shift_of[h] = stats.tile([P, BLOCKS], F32, name="shift", tag="shift")
                row_sum_of[h] = stats.tile([P, BLOCKS], F32, name="row_sum", tag="row_sum")
            qk_t, x_sb = qk_t_of[h], x_of[h]
            s_ps = score_bank([P, SEQ])
            for kb in range(BLOCKS):
                nc.tensor.matmul(
                    out=s_ps[:, kb * P : (kb + 1) * P],
                    lhsT=x_sb[:, kb, ib * P : (ib + 1) * P],
                    rhs=ident_f32[:],
                    is_transpose=True,
                    start=(kb == 0),
                    stop=False,
                )
            nc.tensor.matmul(
                out=s_ps[:],
                lhsT=qk_t[:, ib, :],
                rhs=qk_t[:, BLOCKS:, :].rearrange("d kb p -> d (kb p)"),
                start=False,
                stop=True,
            )
            s_ps_of[(h, ib)] = s_ps

        def row_max(h, ib):
            products = work.tile([P, SEQ], F32, name="products", tag="products")
            nc.vector.tensor_scalar(
                out=products[:],
                in0=s_ps_of[(h, ib)][:],
                scalar1=-SCALE,
                scalar2=None,
                op0=ALU.mult,
                op1=ALU.min,
                accum_out=shift_of[h][:, ib : ib + 1],
            )

        def exponential(h, ib):
            one = slice(ib, ib + 1)
            nc.scalar.activation(
                out=e_of[h][:, ib, :],
                in_=s_ps_of[(h, ib)][:],
                func=ACT.Exp,
                bias=shift_of[h][:, one],
                scale=SCALE,
                accum_out=row_sum_of[h][:, one],
            )

        def transpose_e(h, half):
            e_ps = psum.tile([P, 2, 2, P], F32, name="transpose_bank", tag="transpose_bank", bufs=2)
            e_words = e_of[h][:].rearrange("p ib j -> p (ib j)").bitcast(F32)
            for x in range(2):
                for u in range(2):
                    first = ((2 * half + x) * 2 + u) * P
                    nc.tensor.transpose(e_ps[:, x, u, :], e_words[:, first : first + P], ident_f32[:])
            e_ps_of[(h, half)] = e_ps

        def group_e(h, half):
            if half == 0:
                e_grouped_of[h] = work.tile(
                    [P, BLOCKS, P, 2], F32, name="e_grouped", tag="e_grouped", align_bytes=64
                )
            nc.scalar.copy(
                out=e_grouped_of[h][:, 2 * half : 2 * half + 2, :, :],
                in_=e_ps_of[(h, half)][:].rearrange("p x u m -> p x m u"),
            )

        def quantise_e(h, first=0, stop=BLOCKS):
            if first == 0:
                e_codes = work.tile([P, SEQ], U32, name="e_codes", tag="e_codes", align_bytes=64)
                e_scales = work.tile([P, SEQ], U8, name="e_scales", tag="e_scales", align_bytes=64)
                e_mx_of[h] = (e_codes, e_scales)
            e_codes, e_scales = e_mx_of[h]
            queries = slice(first * P, stop * P)
            nc.vector.quantize_mx(
                out=e_codes[:, queries].bitcast(FP8X4),
                scales=e_scales[:, queries],
                in_=e_grouped_of[h][:, first:stop].rearrange("p ib m u -> p (ib m u)").bitcast(BF16),
            )

        def group_w(h):
            group = max(g for g in range(GROUPS) if GROUP_STARTS[g] <= h)
            w_grouped = work.tile([P, PASSES, HEAD_DIM, PACK], BF16, name="w_grouped", tag="w_grouped", align_bytes=64)
            nc.vector.tensor_copy(
                out=w_grouped[:].rearrange("p g (c i) t -> p g c t i", i=4),
                in_=w_raw_of[group][:, :, :, head_cols(h, GROUP_STARTS[group])].rearrange("p g t (c i) -> p g c t i", i=4),
            )
            w_grouped_of[h] = w_grouped
            if h == GROUP_STOPS[group] - 1 and group + W_BUFFERS < GROUPS:
                load_w(group + W_BUFFERS)

        def quantise_w(h):
            w_codes = work.tile([P, PASSES, HEAD_DIM], U32, name="w_codes", tag="w_codes", align_bytes=64)
            w_scales = work.tile([P, PASSES, HEAD_DIM], U8, name="w_scales", tag="w_scales", align_bytes=64)
            nc.vector.quantize_mx(
                out=w_codes[:].rearrange("p g n -> p (g n)").bitcast(FP8X4),
                scales=w_scales[:].rearrange("p g n -> p (g n)"),
                in_=w_grouped_of[h][:].rearrange("p g n t -> p (g n t)"),
            )
            w_mx_of[h] = (w_codes, w_scales)

        def project_value(h, part):
            w_codes, w_scales = w_mx_of[h]
            if part == 0:
                v_ps_of[h] = psum.tile([P, BLOCKS, HEAD_DIM], F32, name="v_ps", tag="v_ps")
            v_ps = v_ps_of[h]
            for n in range(*PROJECT_PARTS[part]):
                t, g = divmod(n, PASSES)
                nc.tensor.matmul_mx(
                    out=v_ps[:, t, :],
                    lhsT=hs_codes[:, t, g, :].bitcast(FP8X4),
                    lhsT_scale=hs_scales[:, t, g, :],
                    rhs=w_codes[:, g, :].bitcast(FP8X4),
                    rhs_scale=w_scales[:, g, :],
                    start=(g == 0),
                    stop=(g == PASSES - 1),
                )

        def group_value(h):
            v_grouped = work.tile([P, HEAD_DIM, PACK], BF16, name="v_grouped", tag="v_grouped", align_bytes=64)
            bias = bias_sb[:, head_cols(h)].unsqueeze(2).to_broadcast([P, HEAD_DIM, PACK])
            nc.vector.tensor_tensor(
                out=v_grouped[:], in0=v_ps_of[h][:].rearrange("p t d -> p d t"), in1=bias, op=ALU.add
            )
            v_grouped_of[h] = v_grouped

        def quantise_value(h):
            v_codes = work.tile([P, HEAD_DIM], U32, name="v_codes", tag="v_codes", align_bytes=64)
            v_scales = work.tile([P, HEAD_DIM], U8, name="v_scales", tag="v_scales", align_bytes=64)
            nc.vector.quantize_mx(
                out=v_codes[:].bitcast(FP8X4),
                scales=v_scales[:],
                in_=v_grouped_of[h][:].rearrange("p d t -> p (d t)"),
            )
            v_mx_of[h] = (v_codes, v_scales)

        def context(h, bank, first=0, stop=BLOCKS):
            e_codes, e_scales = e_mx_of[h]
            v_codes, v_scales = v_mx_of[h]
            ctx_ps = bank([P, stop - first, HEAD_DIM])
            for ib in range(first, stop):
                queries = slice(ib * P, (ib + 1) * P)
                nc.tensor.matmul_mx(
                    out=ctx_ps[:, ib - first, :],
                    lhsT=e_codes[:, queries].bitcast(FP8X4),
                    lhsT_scale=e_scales[:, queries],
                    rhs=v_codes[:].bitcast(FP8X4),
                    rhs_scale=v_scales[:],
                    start=True,
                    stop=True,
                )
            ctx_ps_of[(h, first)] = ctx_ps

        inv_sum_of = {}

        def invert_sums(h):
            inv_sum = stats.tile([P, BLOCKS], F32, name="inv_sum", tag="inv_sum")
            nc.vector.reciprocal(out=inv_sum[:], in_=row_sum_of[h][:])
            inv_sum_of[h] = inv_sum

        def divide(h, stop=BLOCKS):
            out_sb = work.tile([P, BLOCKS, HEAD_DIM], F32, name="out_sb", tag="out_sb")
            for ib in range(stop):
                nc.scalar.activation(
                    out=out_sb[:, ib, :],
                    in_=ctx_ps_of[(h, 0)][:, ib, :],
                    func=ACT.Copy,
                    scale=inv_sum_of[h][:, ib : ib + 1],
                )
            nc.sync.dma_start(out=out_rows[:, 0:stop, head_cols(h)], in_=out_sb[:, 0:stop, :])

        def divide_rest(h, first):
            rest = BLOCKS - first
            rest_sb = work.tile([P, rest, HEAD_DIM], F32, name="rest_sb", tag="rest_sb", bufs=1)
            nc.vector.tensor_tensor(
                out=rest_sb[:],
                in0=ctx_ps_of[(h, first)][:],
                in1=inv_sum_of[h][:, first:].unsqueeze(2).to_broadcast([P, rest, HEAD_DIM]),
                op=ALU.mult,
            )
            nc.sync.dma_start(out=out_rows[:, first:, head_cols(h)], in_=rest_sb[:])

        last = HEADS - 1

        def run(slot, offset, piece, *args, heads=range(HEADS)):
            h, rest = divmod(slot - offset, BLOCKS)
            if rest == 0 and h in heads:
                piece(h, *args)

        def run_last(slot, offset, piece, *args):
            if slot - offset == BLOCKS * last:
                piece(last, *args)

        def run_block(slot, offset, piece):
            if 0 <= slot - offset < BLOCKS:
                piece(slot - offset)

        added_terms(0, engine=nc.vector)
        transpose_query_and_key(0)
        keep_clock(3)
        copy_query_and_key(0)

        for slot in range(BLOCKS * HEADS + LAST_OFFSET + 1):
            run(slot, -4, added_terms)

            for ib in range(BLOCKS):
                run(slot, ib, score_matmul, ib)
            for part in range(len(PROJECT_PARTS)):
                run(slot, 5 + part, project_value, part)
            run(slot, 12, context, context_bank, heads=range(last))
            run_last(slot, 11, context, score_bank, 0, 2)
            run_last(slot, 12, context, score_bank, 2, BLOCKS)
            if slot < 5:
                keep_clock(1)
            run(slot, -4, transpose_query_and_key)
            run(slot, 5, transpose_e, 0)
            run(slot, 7, transpose_e, 1)
            run_block(slot, 0, transpose_hidden_states)

            for ib in range(BLOCKS):
                run(slot, ib + 1, row_max, ib)
                run(slot, ib + 2, exponential, ib)
            run_block(slot, 1, group_hidden_states)
            run(slot, 8, group_value)
            run(slot, 8, invert_sums)
            run(slot, 10, quantise_value)
            if slot == 3:
                group_w(0)
            elif slot != 2:
                run(slot, 2, group_w)
            run(slot, 10, quantise_e, heads=range(last))
            run_last(slot, 8, quantise_e, 0, 2)
            run_last(slot, 10, quantise_e, 2, BLOCKS)
            if slot == 4:
                quantise_w(0)
            elif slot != 3:
                run(slot, 3, quantise_w)
            run_block(slot, 2, quantise_hidden_states)

            run(slot, -3, copy_query_and_key)
            run(slot, 6, group_e, 0)
            run(slot, 8, group_e, 1)
            run(slot, 13, divide, heads=range(last))
            run_last(slot, 12, divide, 2)
            run_last(slot, 13, divide_rest, 2)
